import numpy as np
import ml_dtypes


def mxq(x, axis, fmt="e4m3"):
    dtype, down = {"e4m3": (ml_dtypes.float8_e4m3fn, 7), "e5m2": (ml_dtypes.float8_e5m2, 14)}[fmt]
    v = np.moveaxis(np.asarray(x, np.float32).astype(ml_dtypes.bfloat16).astype(np.float64), axis, -1)
    blocks = v.reshape(v.shape[:-1] + (-1, 32))
    amax = np.abs(blocks).max(-1, keepdims=True)
    byte = np.maximum(np.where(amax > 0, np.frexp(amax)[1] - 1 + 127, 0) - down, 1)
    scale = np.exp2(byte - 127.0)
    codes = (blocks / scale).astype(np.float32).astype(dtype).astype(np.float64)
    return np.moveaxis((codes * scale).reshape(v.shape), -1, axis)


WIDE = False


def mx_kscale(k):
    if not WIDE:
        return np.ones(k)
    levels = np.array([10, -10, 5, -5, 0])
    a = np.random.permutation(np.resize(levels, k // 512 * 4)).reshape(k // 512, 4)
    idx = np.arange(k)
    return np.exp2(a[idx // 512, idx % 128 // 32])


BF16 = ml_dtypes.bfloat16


def bf(x):
    return np.asarray(x, np.float32).astype(BF16)


def f64(x):
    return np.asarray(x).astype(np.float64)


B, C, H, W = 64, 1024, 10, 10
RAT_S = 0.05
POOL = 5
EPS = 1e-12


def l2norm_c(x):
    n = np.sqrt(np.sum(x * x, axis=1, keepdims=True))
    return x / np.maximum(n, EPS)


def zero_window_mask(h1, w1, h2, w2):
    sr, sc = h1 * RAT_S, w1 * RAT_S
    cent_r = np.repeat(np.arange(h1, dtype=np.float64), w1)
    cent_c = np.tile(np.arange(w1, dtype=np.float64), h1)
    ind_r = np.arange(h2, dtype=np.float64)
    ind_c = np.arange(w2, dtype=np.float64)
    g_r = np.exp(-((ind_r[None, :] - cent_r[:, None]) ** 2) / (2.0 * sr * sr))
    g_c = np.exp(-((ind_c[None, :] - cent_c[:, None]) ** 2) / (2.0 * sc * sc))
    return 1.0 - g_r[:, :, None] * g_c[:, None, :]


def softmax(s, axis):
    e = np.exp(s - s.max(axis=axis, keepdims=True))
    return e / e.sum(axis=axis, keepdims=True)


def pool5(x):
    b, ch, hh, ww = x.shape
    return x.reshape(b, ch, POOL, hh // POOL, POOL, ww // POOL).max(axis=(3, 5))


def setup_inputs():
    base = np.random.standard_normal((B, C, H, W))
    near = np.roll(base, H // 10, axis=2)
    far = np.roll(base, (H // 2, W // 2), axis=(2, 3))
    other = 0.5 * (base + near + far) + 0.5 * np.random.standard_normal((B, C, H, W))
    gp = np.exp(0.5 * np.random.standard_normal((B, 1, H, W)))
    gq = np.exp(0.5 * np.random.standard_normal((B, 1, H, W)))
    ks = mx_kscale(C)
    kc = ks[None, :, None, None]
    comp = np.sqrt(np.mean(ks ** 2) * np.mean(1.0 / ks ** 2))
    return {"xp": bf(base * gp * kc), "xq": bf(other * gq / kc),
            "alpha": bf(2.2 * np.log(H * W) * (1.0 + 0.05 * np.random.standard_normal(1)) * comp)}


def reference(xp, xq, alpha):
    xp, xq = f64(xp), f64(xq)
    b, c, h1, w1 = xp.shape
    h2, w2 = xq.shape[2], xq.shape[3]
    a = f64(alpha).reshape(())
    xpn = l2norm_c(xp)
    xqn = l2norm_c(xq)
    aff = mxq(xpn.reshape(b, c, h1 * w1), 1, "e4m3").transpose(0, 2, 1) @ mxq(xqn.reshape(b, c, h2 * w2), 1, "e4m3")
    mask = zero_window_mask(h1, w1, h2, w2)
    aff = (aff.reshape(b, h1 * w1, h2, w2) * mask[None]).reshape(b, h1 * w1, h2 * w2)
    s = aff * a
    x_c = softmax(s, -1) * softmax(s, -2)
    xc5 = x_c.reshape(b, h1, w1, h2, w2)
    xr_q = xc5.transpose(0, 3, 4, 1, 2).reshape(b, h2 * w2, h1, w1)
    valq = pool5(xr_q).reshape(b, h2, w2, POOL * POOL).transpose(0, 3, 1, 2)
    xr_p = x_c.reshape(b, h1 * w1, h2, w2)
    valp = pool5(xr_p).reshape(b, h1, w1, POOL * POOL).transpose(0, 3, 1, 2)
    x_soft_q = x_c.reshape(b, h1 * w1, h2, w2)
    x_soft_p = x_soft_q.transpose(0, 2, 3, 1).reshape(b, h2 * w2, h1, w1)
    return valp, valq, x_soft_p, x_soft_q

@@ -1,0 +1,221 @@
+import concourse.mybir as mybir
+from concourse.masks import make_identity
+
+FLOPS = 2 * 64 * 100 * 100 * 1024
+
+BF16 = mybir.dt.bfloat16
+F32 = mybir.dt.float32
+I32 = mybir.dt.int32
+U32 = mybir.dt.uint32
+U8 = mybir.dt.uint8
+FP8X4 = mybir.dt.float8_e4m3fn_x4
+ALU = mybir.AluOpType
+ACT = mybir.ActivationFunctionType
+AX = mybir.AxisListType
+
+P = 128
+B = 64
+POS = 100
+UB = 4
+NU = B // UB
+CH = 8
+XW = UB * CH * POS
+PADW = P - POS
+EW = UB * POS
+NX = 6
+NY = 3
+NE = 3
+EPS2 = 1e-24
+
+
+def tile_corr_t_kernel(tc, xp, xq, alpha, out_0, out_1, out_2, out_3):
+    nc = tc.nc
+    with tc.tile_pool(name="const", bufs=1) as const, \
+            tc.tile_pool(name="fixed", bufs=1) as fixed, \
+            tc.tile_pool(name="work", bufs=3) as work, \
+            tc.tile_pool(name="codes", bufs=4) as cpool, \
+            tc.psum_pool(name="pxt", bufs=3) as pxt, \
+            tc.psum_pool(name="prb", bufs=2) as prb, \
+            tc.psum_pool(name="pep", bufs=3) as pep:
+
+        ident_b = const.tile([P, P], BF16, name="ident_b")
+        make_identity(nc, ident_b[:])
+        ident_f = const.tile([P, P], F32, name="ident_f")
+        make_identity(nc, ident_f[:])
+        neg_half = const.tile([P, UB], F32, name="neg_half")
+        nc.gpsimd.memset(neg_half[:], -0.5)
+
+        xt = [fixed.tile([P, XW + 32], BF16, name="x%d" % k) for k in range(NX)]
+        yt = [fixed.tile([P, UB, 2, P, 4], BF16, name="y%d" % k, align_bytes=64) for k in range(NY)]
+        sa_t = [fixed.tile([P, EW + PADW], F32, name="sa%d" % k) for k in range(NE)]
+        f2_t = [fixed.tile([P, EW + PADW], F32, name="f2%d" % k) for k in range(NE)]
+        xa_t = [fixed.tile([P, EW + PADW], F32, name="xa%d" % k) for k in range(NE)]
+        pl_t = [fixed.tile([P, 2, P], F32, name="pl%d" % k) for k in range(NE)]
+        for k in range(NX):
+            nc.gpsimd.memset(xt[k][:, XW:XW + 32], 0.0)
+        for k in range(NY):
+            nc.gpsimd.memset(yt[k][:], 0.0)
+        for k in range(NE):
+            nc.gpsimd.memset(sa_t[k][:, EW:EW + PADW], 0.0)
+            nc.gpsimd.memset(f2_t[k][:, EW:EW + PADW], 0.0)
+            nc.gpsimd.memset(xa_t[k][:, EW:EW + PADW], 0.0)
+            nc.gpsimd.memset(pl_t[k][:], 0.0)
+
+        a_bf = const.tile([P, 1], BF16, name="a_bf")
+        nc.sync.dma_start(out=a_bf[:], in_=alpha.partition_broadcast(P))
+        pi = const.tile([P, 1], I32, name="pi")
+        nc.gpsimd.iota(pi[:], pattern=[[0, 1]], base=0, channel_multiplier=1)
+        ti = const.tile([P, 12], I32, name="ti")
+        nc.gpsimd.iota(ti[:], pattern=[[10, 12]], base=10, channel_multiplier=0)
+        ki = const.tile([P, 10], I32, name="ki")
+        nc.gpsimd.iota(ki[:], pattern=[[1, 10]], base=0, channel_multiplier=0)
+        pf = const.tile([P, 1], F32, name="pf")
+        nc.vector.tensor_copy(out=pf[:], in_=pi[:])
+        tf = const.tile([P, 12], F32, name="tf")
+        nc.vector.tensor_copy(out=tf[:], in_=ti[:])
+        kf = const.tile([P, 10], F32, name="kf")
+        nc.vector.tensor_copy(out=kf[:], in_=ki[:])
+        ge = const.tile([P, 12], F32, name="ge")
+        nc.vector.tensor_scalar(out=ge[:], in0=tf[:], scalar1=pf[:, 0:1], scalar2=None, op0=ALU.is_le)
+        irow = const.tile([P, 1], F32, name="irow")
+        nc.vector.tensor_reduce(out=irow[:], in_=ge[:], axis=AX.X, op=ALU.add)
+        jcol = const.tile([P, 1], F32, name="jcol")
+        nc.vector.scalar_tensor_tensor(out=jcol[:], in0=irow[:], scalar=-10.0, in1=pf[:],
+                                       op0=ALU.mult, op1=ALU.add)
+        dd = const.tile([P, 2, 10], F32, name="dd")
+        nc.vector.tensor_scalar(out=dd[:, 0, :], in0=kf[:], scalar1=irow[:, 0:1], scalar2=None, op0=ALU.subtract)
+        nc.vector.tensor_scalar(out=dd[:, 1, :], in0=kf[:], scalar1=jcol[:, 0:1], scalar2=None, op0=ALU.subtract)
+        d2 = const.tile([P, 2, 10], F32, name="d2")
+        nc.vector.tensor_tensor(out=d2[:], in0=dd[:], in1=dd[:], op=ALU.mult)
+        gg = const.tile([P, 2, 10], F32, name="gg")
+        nc.scalar.activation(out=gg[:], in_=d2[:], func=ACT.Exp, scale=-2.0)
+        g2 = const.tile([P, 10, 10], F32, name="g2")
+        nc.vector.tensor_tensor(out=g2[:],
+                                in0=gg[:, 0, :].unsqueeze(2).to_broadcast([P, 10, 10]),
+                                in1=gg[:, 1, :].unsqueeze(1).to_broadcast([P, 10, 10]),
+                                op=ALU.mult)
+        a_f = const.tile([P, 1], F32, name="a_f")
+        nc.vector.tensor_copy(out=a_f[:], in_=a_bf[:])
+        wm1 = const.tile([P, POS], F32, name="wm1")
+        nc.vector.tensor_scalar(out=wm1[:], in0=g2[:].rearrange("p k l -> p (k l)"), scalar1=1.0,
+                                scalar2=None, op0=ALU.subtract)
+        wneg = const.tile([P, POS], F32, name="wneg")
+        nc.vector.tensor_scalar(out=wneg[:], in0=wm1[:], scalar1=a_f[:, 0:1], scalar2=None, op0=ALU.mult)
+
+        junk = const.tile([P, CH * P], BF16, name="junk")
+
+        for u in range(NU):
+            b0 = u * UB
+            quant = []
+            for op_i, src in enumerate((xp, xq)):
+                x = xt[(2 * u + op_i) % NX]
+                y = yt[(2 * u + op_i) % NY]
+                nc.sync.dma_start(
+                    out=x[:, 0:XW].rearrange("p (n f) -> p n f", n=2 * UB),
+                    in_=src[b0:b0 + UB].rearrange("b (g p j) h w -> p (b g) (j h w)", g=2, p=P, j=4),
+                )
+                n2 = work.tile([P, UB], F32, name="n2")
+                for i in range(UB):
+                    xT = pxt.tile([P, CH * P], BF16, name="xT")
+                    for t in range(CH):
+                        c0 = (i * CH + t) * POS
+                        nc.tensor.transpose(xT[:, t * P:(t + 1) * P], x[:, c0:c0 + P], ident_b[:])
+                    nc.scalar.activation(out=junk[:], in_=xT[:], func=ACT.Square,
+                                         accum_out=n2[:, i:i + 1])
+                n2c = work.tile([P, UB], F32, name="n2c")
+                nc.gpsimd.tensor_scalar_max(out=n2c[:], in0=n2[:], scalar1=EPS2)
+                rn = work.tile([P, UB], F32, name="rn")
+                nc.gpsimd.tensor_tensor(out=rn[:], in0=n2c[:], in1=neg_half[:], op=ALU.pow)
+                rb = prb.tile([P, UB, P], F32, name="rb")
+                for i in range(UB):
+                    nc.tensor.transpose(rb[:, i, :], rn[:, i:i + 1].to_broadcast([P, P]), ident_f[:])
+                for i in range(UB):
+                    nc.vector.tensor_tensor(
+                        out=y[:, i, :, 0:POS, :],
+                        in0=x[:, i * CH * POS:(i + 1) * CH * POS].rearrange(
+                            "p (g j w) -> p g w j", g=2, j=4),
+                        in1=rb[:, i, 0:POS].unsqueeze(1).unsqueeze(3).to_broadcast([P, 2, POS, 4]),
+                        op=ALU.mult,
+                    )
+                cw = cpool.tile([P, UB * 2 * P], U32, name="cw", align_bytes=64)
+                cs = cpool.tile([P, UB * 2 * P], U8, name="cs", align_bytes=64)
+                nc.vector.quantize_mx(out=cw[:].bitcast(FP8X4), scales=cs[:],
+                                      in_=y[:].rearrange("p b g w j -> p (b g w j)"))
+                quant.append((cw, cs))
+
+            (cwp, csp), (cwq, csq) = quant
+            aff = pep.tile([P, UB, P], F32, name="aff", tag="ep")
+            for i in range(UB):
+                for g in range(2):
+                    cols = slice((i * 2 + g) * P, (i * 2 + g + 1) * P)
+                    nc.tensor.matmul_mx(out=aff[:, i, :],
+                                        lhsT=cwp[:, cols].bitcast(FP8X4), lhsT_scale=csp[:, cols],
+                                        rhs=cwq[:, cols].bitcast(FP8X4), rhs_scale=csq[:, cols],
+                                        start=(g == 0), stop=(g == 1))
+
+            sa = sa_t[u % NE]
+            f2 = f2_t[u % NE]
+            xa = xa_t[u % NE]
+            pl = pl_t[u % NE]
+            nc.vector.tensor_tensor(out=sa[:, 0:EW].rearrange("p (b q) -> p b q", b=UB),
+                                    in0=aff[:, :, 0:POS],
+                                    in1=wneg[:].unsqueeze(1).to_broadcast([P, UB, POS]),
+                                    op=ALU.mult)
+            sb = pep.tile([P, UB, P], F32, name="sb", tag="ep")
+            for i in range(UB):
+                nc.tensor.transpose(sb[:, i, :], sa[:, i * POS:i * POS + P], ident_f[:])
+            nm = work.tile([P, 2 * UB], F32, name="nm")
+            nc.vector.tensor_reduce(out=nm[:, 0:UB], in_=sa[:, 0:EW].rearrange("p (b q) -> p b q", b=UB),
+                                    axis=AX.X, op=ALU.min)
+            nc.vector.tensor_reduce(out=nm[:, UB:2 * UB], in_=sb[:, :, 0:POS], axis=AX.X, op=ALU.min)
+            e1 = work.tile([P, EW], F32, name="e1")
+            e2 = work.tile([P, EW], F32, name="e2")
+            sm = work.tile([P, 2 * UB], F32, name="sm")
+            for i in range(UB):
+                nc.scalar.activation(out=e1[:, i * POS:(i + 1) * POS], in_=sa[:, i * POS:(i + 1) * POS],
+                                     func=ACT.Exp, bias=nm[:, i:i + 1], scale=-1.0,
+                                     accum_out=sm[:, i:i + 1])
+            for i in range(UB):
+                nc.scalar.activation(out=e2[:, i * POS:(i + 1) * POS], in_=sb[:, i, 0:POS],
+                                     func=ACT.Exp, bias=nm[:, UB + i:UB + i + 1], scale=-1.0,
+                                     accum_out=sm[:, UB + i:UB + i + 1])
+            rs = work.tile([P, 2 * UB], F32, name="rs")
+            nc.vector.reciprocal(out=rs[:], in_=sm[:])
+            for i in range(UB):
+                nc.gpsimd.tensor_scalar(out=f2[:, i * POS:(i + 1) * POS], in0=e2[:, i * POS:(i + 1) * POS],
+                                        scalar1=rs[:, UB + i:UB + i + 1], scalar2=1.0,
+                                        op0=ALU.mult, op1=ALU.mult)
+            f2T = pep.tile([P, UB, P], F32, name="f2T", tag="ep")
+            for i in range(UB):
+                nc.tensor.transpose(f2T[:, i, :], f2[:, i * POS:i * POS + P], ident_f[:])
+            for i in range(UB):
+                nc.vector.scalar_tensor_tensor(out=xa[:, i * POS:(i + 1) * POS],
+                                               in0=e1[:, i * POS:(i + 1) * POS],
+                                               scalar=rs[:, i:i + 1],
+                                               in1=f2T[:, i, 0:POS],
+                                               op0=ALU.mult, op1=ALU.mult)
+            nc.sync.dma_start(out=out_3[b0:b0 + UB].rearrange("b p k l -> p b (k l)"),
+                              in_=xa[0:POS, 0:EW].rearrange("p (b q) -> p b q", b=UB))
+            xbT = pep.tile([P, UB, P], F32, name="xbT", tag="ep")
+            for i in range(UB):
+                nc.tensor.transpose(xbT[:, i, :], xa[:, i * POS:i * POS + P], ident_f[:])
+            xb = work.tile([P, EW], F32, name="xb")
+            nc.scalar.copy(out=xb[:].rearrange("p (b q) -> p b q", b=UB), in_=xbT[:, :, 0:POS])
+            nc.sync.dma_start(out=out_2[b0:b0 + UB].rearrange("b q i j -> q b (i j)"),
+                              in_=xb[0:POS, :].rearrange("p (b q) -> p b q", b=UB))
+            for side, srcx in enumerate((xa, xb)):
+                pair = srcx[:, 0:EW].rearrange("p (n two) -> p n two", two=2)
+                hm = work.tile([P, EW // 2], F32, name="hm")
+                nc.vector.tensor_tensor(out=hm[:], in0=pair[:, :, 0], in1=pair[:, :, 1], op=ALU.max)
+                hv = hm[:].rearrange("p (m dk t) -> p m dk t", dk=2, t=5)
+                nc.vector.tensor_tensor(out=pl[:, side, 0:UB * 25].rearrange("p (m t) -> p m t", t=5),
+                                        in0=hv[:, :, 0, :], in1=hv[:, :, 1, :], op=ALU.max)
+            plT = pep.tile([P, 2, P], F32, name="plT", tag="ep")
+            for side in range(2):
+                nc.tensor.transpose(plT[:, side, :], pl[:, side, :], ident_f[:])
+            vals = work.tile([P, 2, POS], F32, name="vals")
+            nc.scalar.copy(out=vals[:], in_=plT[:, :, 0:POS])
+            nc.sync.dma_start(out=out_0[b0:b0 + UB].rearrange("b c i j -> (b c) (i j)"),
+                              in_=vals[0:UB * 25, 0, :])
+            nc.sync.dma_start(out=out_1[b0:b0 + UB].rearrange("b c k l -> (b c) (k l)"),
+                              in_=vals[0:UB * 25, 1, :])

@@ -22,47 +22,47 @@ CH = 8
 XW = UB * CH * POS
 PADW = P - POS
 EW = UB * POS
-NX = 6
-NY = 3
-NE = 3
+NXB = 4
 EPS2 = 1e-24
+PP = 0
+QQ = 1
 
 
 def tile_corr_t_kernel(tc, xp, xq, alpha, out_0, out_1, out_2, out_3):
     nc = tc.nc
     with tc.tile_pool(name="const", bufs=1) as const, \
             tc.tile_pool(name="fixed", bufs=1) as fixed, \
-            tc.tile_pool(name="work", bufs=3) as work, \
-            tc.tile_pool(name="codes", bufs=4) as cpool, \
+            tc.tile_pool(name="work", bufs=2) as work, \
+            tc.tile_pool(name="small", bufs=4) as small, \
             tc.psum_pool(name="pxt", bufs=3) as pxt, \
-            tc.psum_pool(name="prb", bufs=2) as prb, \
-            tc.psum_pool(name="pep", bufs=3) as pep:
-
+            tc.psum_pool(name="pone", bufs=1) as pone:
         ident_b = const.tile([P, P], BF16, name="ident_b")
         make_identity(nc, ident_b[:])
         ident_f = const.tile([P, P], F32, name="ident_f")
         make_identity(nc, ident_f[:])
         neg_half = const.tile([P, UB], F32, name="neg_half")
         nc.gpsimd.memset(neg_half[:], -0.5)
+        wneg = const.tile([P, POS], F32, name="wneg")
+        junk = const.tile([P, CH * P], BF16, name="junk")
 
-        xt = [fixed.tile([P, XW + 32], BF16, name="x%d" % k) for k in range(NX)]
-        yt = [fixed.tile([P, UB, 2, P, 4], BF16, name="y%d" % k, align_bytes=64) for k in range(NY)]
-        sa_t = [fixed.tile([P, EW + PADW], F32, name="sa%d" % k) for k in range(NE)]
-        f2_t = [fixed.tile([P, EW + PADW], F32, name="f2%d" % k) for k in range(NE)]
-        xa_t = [fixed.tile([P, EW + PADW], F32, name="xa%d" % k) for k in range(NE)]
-        pl_t = [fixed.tile([P, 2, P], F32, name="pl%d" % k) for k in range(NE)]
-        for k in range(NX):
-            nc.gpsimd.memset(xt[k][:, XW:XW + 32], 0.0)
-        for k in range(NY):
-            nc.gpsimd.memset(yt[k][:], 0.0)
-        for k in range(NE):
+        xt = [[fixed.tile([P, XW + 32], BF16, name="x%d_%d" % (o, k)) for k in range(NXB)] for o in range(2)]
+        yt = [fixed.tile([P, UB, 2, P, 4], BF16, name="y%d" % o, align_bytes=64) for o in range(2)]
+        sa_t = [fixed.tile([P, EW + PADW], F32, name="sa%d" % k) for k in range(2)]
+        f2_t = [fixed.tile([P, EW + PADW], F32, name="f2%d" % k) for k in range(2)]
+        xa_t = [fixed.tile([P, EW + PADW], F32, name="xa%d" % k) for k in range(2)]
+        pl_t = [fixed.tile([P, 2, P], F32, name="pl%d" % k) for k in range(2)]
+        for o in range(2):
+            for k in range(NXB):
+                nc.vector.memset(xt[o][k][:, XW:XW + 32], 0.0)
+            nc.vector.memset(yt[o][:, :, :, POS:P, :], 0.0)
+        for k in range(2):
             nc.gpsimd.memset(sa_t[k][:, EW:EW + PADW], 0.0)
             nc.gpsimd.memset(f2_t[k][:, EW:EW + PADW], 0.0)
             nc.gpsimd.memset(xa_t[k][:, EW:EW + PADW], 0.0)
             nc.gpsimd.memset(pl_t[k][:], 0.0)
 
         a_bf = const.tile([P, 1], BF16, name="a_bf")
-        nc.sync.dma_start(out=a_bf[:], in_=alpha.partition_broadcast(P))
+        nc.scalar.dma_start(out=a_bf[:], in_=alpha.partition_broadcast(P))
         pi = const.tile([P, 1], I32, name="pi")
         nc.gpsimd.iota(pi[:], pattern=[[0, 1]], base=0, channel_multiplier=1)
         ti = const.tile([P, 12], I32, name="ti")
@@ -83,8 +83,10 @@ def tile_corr_t_kernel(tc, xp, xq, alpha, out_0, out_1, out_2, out_3):
         nc.vector.scalar_tensor_tensor(out=jcol[:], in0=irow[:], scalar=-10.0, in1=pf[:],
                                        op0=ALU.mult, op1=ALU.add)
         dd = const.tile([P, 2, 10], F32, name="dd")
-        nc.vector.tensor_scalar(out=dd[:, 0, :], in0=kf[:], scalar1=irow[:, 0:1], scalar2=None, op0=ALU.subtract)
-        nc.vector.tensor_scalar(out=dd[:, 1, :], in0=kf[:], scalar1=jcol[:, 0:1], scalar2=None, op0=ALU.subtract)
+        nc.vector.tensor_scalar(out=dd[:, 0, :], in0=kf[:], scalar1=irow[:, 0:1], scalar2=None,
+                                op0=ALU.subtract)
+        nc.vector.tensor_scalar(out=dd[:, 1, :], in0=kf[:], scalar1=jcol[:, 0:1], scalar2=None,
+                                op0=ALU.subtract)
         d2 = const.tile([P, 2, 10], F32, name="d2")
         nc.vector.tensor_tensor(out=d2[:], in0=dd[:], in1=dd[:], op=ALU.mult)
         gg = const.tile([P, 2, 10], F32, name="gg")
@@ -99,52 +101,89 @@ def tile_corr_t_kernel(tc, xp, xq, alpha, out_0, out_1, out_2, out_3):
         wm1 = const.tile([P, POS], F32, name="wm1")
         nc.vector.tensor_scalar(out=wm1[:], in0=g2[:].rearrange("p k l -> p (k l)"), scalar1=1.0,
                                 scalar2=None, op0=ALU.subtract)
-        wneg = const.tile([P, POS], F32, name="wneg")
         nc.vector.tensor_scalar(out=wneg[:], in0=wm1[:], scalar1=a_f[:, 0:1], scalar2=None, op0=ALU.mult)
 
-        junk = const.tile([P, CH * P], BF16, name="junk")
 
-        for u in range(NU):
-            b0 = u * UB
-            quant = []
-            for op_i, src in enumerate((xp, xq)):
-                x = xt[(2 * u + op_i) % NX]
-                y = yt[(2 * u + op_i) % NY]
-                nc.sync.dma_start(
-                    out=x[:, 0:XW].rearrange("p (n f) -> p n f", n=2 * UB),
-                    in_=src[b0:b0 + UB].rearrange("b (g p j) h w -> p (b g) (j h w)", g=2, p=P, j=4),
-                )
-                n2 = work.tile([P, UB], F32, name="n2")
-                for i in range(UB):
-                    xT = pxt.tile([P, CH * P], BF16, name="xT")
-                    for t in range(CH):
-                        c0 = (i * CH + t) * POS
-                        nc.tensor.transpose(xT[:, t * P:(t + 1) * P], x[:, c0:c0 + P], ident_b[:])
-                    nc.scalar.activation(out=junk[:], in_=xT[:], func=ACT.Square,
-                                         accum_out=n2[:, i:i + 1])
-                n2c = work.tile([P, UB], F32, name="n2c")
-                nc.gpsimd.tensor_scalar_max(out=n2c[:], in0=n2[:], scalar1=EPS2)
-                rn = work.tile([P, UB], F32, name="rn")
-                nc.gpsimd.tensor_tensor(out=rn[:], in0=n2c[:], in1=neg_half[:], op=ALU.pow)
-                rb = prb.tile([P, UB, P], F32, name="rb")
-                for i in range(UB):
-                    nc.tensor.transpose(rb[:, i, :], rn[:, i:i + 1].to_broadcast([P, P]), ident_f[:])
-                for i in range(UB):
-                    nc.vector.tensor_tensor(
-                        out=y[:, i, :, 0:POS, :],
-                        in0=x[:, i * CH * POS:(i + 1) * CH * POS].rearrange(
-                            "p (g j w) -> p g w j", g=2, j=4),
-                        in1=rb[:, i, 0:POS].unsqueeze(1).unsqueeze(3).to_broadcast([P, 2, POS, 4]),
-                        op=ALU.mult,
-                    )
-                cw = cpool.tile([P, UB * 2 * P], U32, name="cw", align_bytes=64)
-                cs = cpool.tile([P, UB * 2 * P], U8, name="cs", align_bytes=64)
-                nc.vector.quantize_mx(out=cw[:].bitcast(FP8X4), scales=cs[:],
-                                      in_=y[:].rearrange("p b g w j -> p (b g w j)"))
-                quant.append((cw, cs))
+        live = {}
 
-            (cwp, csp), (cwq, csq) = quant
-            aff = pep.tile([P, UB, P], F32, name="aff", tag="ep")
+        def ok(k):
+            return 0 <= k < NU
+
+        def img(ap):
+            return ap.rearrange("p (b q) -> p b q", b=UB)
+
+        def load(k, o):
+            if not ok(k):
+                return
+            src = xp if o == PP else xq
+            nc.sync.dma_start(
+                out=xt[o][k % NXB][:, 0:XW].rearrange("p (n f) -> p n f", n=2 * UB),
+                in_=src[k * UB:(k + 1) * UB].rearrange("b (g p j) h w -> p (b g) (j h w)", g=2, p=P, j=4),
+            )
+
+        def tr(k, o, i):
+            if not ok(k):
+                return
+            x = xt[o][k % NXB]
+            xT = pxt.tile([P, CH * P], BF16, name="xT")
+            for t in range(CH):
+                c0 = (i * CH + t) * POS
+                nc.tensor.transpose(xT[:, t * P:(t + 1) * P], x[:, c0:c0 + P], ident_b[:])
+            live[("xT", k, o, i)] = xT
+
+        def sq(k, o, i):
+            if not ok(k):
+                return
+            if i == 0:
+                n2 = small.tile([P, UB], F32, name="n2")
+                live[("n2", k, o)] = n2
+            nc.scalar.activation(out=junk[:], in_=live[("xT", k, o, i)][:], func=ACT.Square,
+                                 accum_out=live[("n2", k, o)][:, i:i + 1])
+
+        def powr(k, o):
+            if not ok(k):
+                return
+            n2c = small.tile([P, UB], F32, name="n2c")
+            nc.gpsimd.tensor_scalar_max(out=n2c[:], in0=live[("n2", k, o)][:], scalar1=EPS2)
+            rn = small.tile([P, UB], F32, name="rn")
+            nc.gpsimd.tensor_tensor(out=rn[:], in0=n2c[:], in1=neg_half[:], op=ALU.pow)
+            live[("rn", k, o)] = rn
+
+        def bcast(k, o):
+            if not ok(k):
+                return
+            rb = pone.tile([P, UB, P], F32, name="rb", tag="rb%d" % o)
+            rn = live[("rn", k, o)]
+            for i in range(UB):
+                nc.tensor.transpose(rb[:, i, :], rn[:, i:i + 1].to_broadcast([P, P]), ident_f[:])
+            live[("rb", k, o)] = rb
+
+        def mult(k, o, i):
+            if not ok(k):
+                return
+            x = xt[o][k % NXB]
+            nc.vector.tensor_tensor(
+                out=yt[o][:, i, :, 0:POS, :],
+                in0=x[:, i * CH * POS:(i + 1) * CH * POS].rearrange("p (g j w) -> p g w j", g=2, j=4),
+                in1=live[("rb", k, o)][:, i, 0:POS].unsqueeze(1).unsqueeze(3).to_broadcast([P, 2, POS, 4]),
+                op=ALU.mult,
+            )
+
+        def quant(k, o):
+            if not ok(k):
+                return
+            cw = work.tile([P, UB * 2 * P], U32, name="cw", tag="cw%d" % o, align_bytes=64)
+            cs = work.tile([P, UB * 2 * P], U8, name="cs", tag="cs%d" % o, align_bytes=64)
+            nc.vector.quantize_mx(out=cw[:].bitcast(FP8X4), scales=cs[:],
+                                  in_=yt[o][:].rearrange("p b g w j -> p (b g w j)"))
+            live[("c", k, o)] = (cw, cs)
+
+        def mx(e):
+            if not ok(e):
+                return
+            cwp, csp = live[("c", e, PP)]
+            cwq, csq = live[("c", e, QQ)]
+            aff = pone.tile([P, UB, P], F32, name="aff", tag="e0")
             for i in range(UB):
                 for g in range(2):
                     cols = slice((i * 2 + g) * P, (i * 2 + g + 1) * P)
@@ -152,25 +191,42 @@ def tile_corr_t_kernel(tc, xp, xq, alpha, out_0, out_1, out_2, out_3):
                                         lhsT=cwp[:, cols].bitcast(FP8X4), lhsT_scale=csp[:, cols],
                                         rhs=cwq[:, cols].bitcast(FP8X4), rhs_scale=csq[:, cols],
                                         start=(g == 0), stop=(g == 1))
+            live[("aff", e)] = aff
 
-            sa = sa_t[u % NE]
-            f2 = f2_t[u % NE]
-            xa = xa_t[u % NE]
-            pl = pl_t[u % NE]
-            nc.vector.tensor_tensor(out=sa[:, 0:EW].rearrange("p (b q) -> p b q", b=UB),
-                                    in0=aff[:, :, 0:POS],
-                                    in1=wneg[:].unsqueeze(1).to_broadcast([P, UB, POS]),
-                                    op=ALU.mult)
-            sb = pep.tile([P, UB, P], F32, name="sb", tag="ep")
+        def mask(e):
+            if not ok(e):
+                return
+            nc.vector.tensor_tensor(out=img(sa_t[e % 2][:, 0:EW]), in0=live[("aff", e)][:, :, 0:POS],
+                                    in1=wneg[:].unsqueeze(1).to_broadcast([P, UB, POS]), op=ALU.mult)
+
+        def turn(e, key, src, tag):
+            dst = pone.tile([P, UB, P], F32, name=key, tag=tag)
             for i in range(UB):
-                nc.tensor.transpose(sb[:, i, :], sa[:, i * POS:i * POS + P], ident_f[:])
-            nm = work.tile([P, 2 * UB], F32, name="nm")
-            nc.vector.tensor_reduce(out=nm[:, 0:UB], in_=sa[:, 0:EW].rearrange("p (b q) -> p b q", b=UB),
-                                    axis=AX.X, op=ALU.min)
-            nc.vector.tensor_reduce(out=nm[:, UB:2 * UB], in_=sb[:, :, 0:POS], axis=AX.X, op=ALU.min)
+                nc.tensor.transpose(dst[:, i, :], src[:, i * POS:i * POS + P], ident_f[:])
+            live[(key, e)] = dst
+
+        def t_sa(e):
+            if ok(e):
+                turn(e, "sb", sa_t[e % 2], "e1")
+
+        def mins(e):
+            if not ok(e):
+                return
+            nm = small.tile([P, 2 * UB], F32, name="nm")
+            nc.vector.tensor_reduce(out=nm[:, 0:UB], in_=img(sa_t[e % 2][:, 0:EW]), axis=AX.X, op=ALU.min)
+            nc.vector.tensor_reduce(out=nm[:, UB:2 * UB], in_=live[("sb", e)][:, :, 0:POS], axis=AX.X,
+                                    op=ALU.min)
+            live[("nm", e)] = nm
+
+        def exps(e):
+            if not ok(e):
+                return
+            nm = live[("nm", e)]
+            sa = sa_t[e % 2]
+            sb = live[("sb", e)]
             e1 = work.tile([P, EW], F32, name="e1")
             e2 = work.tile([P, EW], F32, name="e2")
-            sm = work.tile([P, 2 * UB], F32, name="sm")
+            sm = small.tile([P, 2 * UB], F32, name="sm")
             for i in range(UB):
                 nc.scalar.activation(out=e1[:, i * POS:(i + 1) * POS], in_=sa[:, i * POS:(i + 1) * POS],
                                      func=ACT.Exp, bias=nm[:, i:i + 1], scale=-1.0,
@@ -179,43 +235,134 @@ def tile_corr_t_kernel(tc, xp, xq, alpha, out_0, out_1, out_2, out_3):
                 nc.scalar.activation(out=e2[:, i * POS:(i + 1) * POS], in_=sb[:, i, 0:POS],
                                      func=ACT.Exp, bias=nm[:, UB + i:UB + i + 1], scale=-1.0,
                                      accum_out=sm[:, UB + i:UB + i + 1])
-            rs = work.tile([P, 2 * UB], F32, name="rs")
-            nc.vector.reciprocal(out=rs[:], in_=sm[:])
+            live[("e1", e)] = e1
+            live[("e2", e)] = e2
+            live[("sm", e)] = sm
+
+        def recip(e):
+            if not ok(e):
+                return
+            rs = small.tile([P, 2 * UB], F32, name="rs")
+            nc.vector.reciprocal(out=rs[:], in_=live[("sm", e)][:])
+            live[("rs", e)] = rs
+
+        def f2s(e):
+            if not ok(e):
+                return
+            rs = live[("rs", e)]
+            e2 = live[("e2", e)]
             for i in range(UB):
-                nc.gpsimd.tensor_scalar(out=f2[:, i * POS:(i + 1) * POS], in0=e2[:, i * POS:(i + 1) * POS],
+                nc.gpsimd.tensor_scalar(out=f2_t[e % 2][:, i * POS:(i + 1) * POS],
+                                        in0=e2[:, i * POS:(i + 1) * POS],
                                         scalar1=rs[:, UB + i:UB + i + 1], scalar2=1.0,
                                         op0=ALU.mult, op1=ALU.mult)
-            f2T = pep.tile([P, UB, P], F32, name="f2T", tag="ep")
+
+        def t_f2(e):
+            if ok(e):
+                turn(e, "f2T", f2_t[e % 2], "e2")
+
+        def stt(e):
+            if not ok(e):
+                return
+            rs = live[("rs", e)]
+            e1 = live[("e1", e)]
+            f2T = live[("f2T", e)]
             for i in range(UB):
-                nc.tensor.transpose(f2T[:, i, :], f2[:, i * POS:i * POS + P], ident_f[:])
-            for i in range(UB):
-                nc.vector.scalar_tensor_tensor(out=xa[:, i * POS:(i + 1) * POS],
-                                               in0=e1[:, i * POS:(i + 1) * POS],
-                                               scalar=rs[:, i:i + 1],
-                                               in1=f2T[:, i, 0:POS],
-                                               op0=ALU.mult, op1=ALU.mult)
-            nc.sync.dma_start(out=out_3[b0:b0 + UB].rearrange("b p k l -> p b (k l)"),
-                              in_=xa[0:POS, 0:EW].rearrange("p (b q) -> p b q", b=UB))
-            xbT = pep.tile([P, UB, P], F32, name="xbT", tag="ep")
-            for i in range(UB):
-                nc.tensor.transpose(xbT[:, i, :], xa[:, i * POS:i * POS + P], ident_f[:])
+                nc.vector.scalar_tensor_tensor(out=xa_t[e % 2][:, i * POS:(i + 1) * POS],
+                                               in0=e1[:, i * POS:(i + 1) * POS], scalar=rs[:, i:i + 1],
+                                               in1=f2T[:, i, 0:POS], op0=ALU.mult, op1=ALU.mult)
+
+        def t_xa(e):
+            if not ok(e):
+                return
+            turn(e, "xbT", xa_t[e % 2], "e0")
+            nc.sync.dma_start(out=out_3[e * UB:(e + 1) * UB].rearrange("b p k l -> p b (k l)"),
+                              in_=img(xa_t[e % 2][0:POS, 0:EW]))
+
+        def cp_xb(e):
+            if not ok(e):
+                return
             xb = work.tile([P, EW], F32, name="xb")
-            nc.scalar.copy(out=xb[:].rearrange("p (b q) -> p b q", b=UB), in_=xbT[:, :, 0:POS])
-            nc.sync.dma_start(out=out_2[b0:b0 + UB].rearrange("b q i j -> q b (i j)"),
-                              in_=xb[0:POS, :].rearrange("p (b q) -> p b q", b=UB))
-            for side, srcx in enumerate((xa, xb)):
-                pair = srcx[:, 0:EW].rearrange("p (n two) -> p n two", two=2)
-                hm = work.tile([P, EW // 2], F32, name="hm")
-                nc.vector.tensor_tensor(out=hm[:], in0=pair[:, :, 0], in1=pair[:, :, 1], op=ALU.max)
-                hv = hm[:].rearrange("p (m dk t) -> p m dk t", dk=2, t=5)
-                nc.vector.tensor_tensor(out=pl[:, side, 0:UB * 25].rearrange("p (m t) -> p m t", t=5),
-                                        in0=hv[:, :, 0, :], in1=hv[:, :, 1, :], op=ALU.max)
-            plT = pep.tile([P, 2, P], F32, name="plT", tag="ep")
+            nc.scalar.copy(out=img(xb[:]), in_=live[("xbT", e)][:, :, 0:POS])
+            nc.sync.dma_start(out=out_2[e * UB:(e + 1) * UB].rearrange("b q i j -> q b (i j)"),
+                              in_=img(xb[0:POS, :]))
+            live[("xb", e)] = xb
+
+        def pool(e, side):
+            if not ok(e):
+                return
+            srcx = xa_t[e % 2] if side == 0 else live[("xb", e)]
+            pair = srcx[:, 0:EW].rearrange("p (n two) -> p n two", two=2)
+            hm = work.tile([P, EW // 2], F32, name="hm")
+            nc.vector.tensor_tensor(out=hm[:], in0=pair[:, :, 0], in1=pair[:, :, 1], op=ALU.max)
+            hv = hm[:].rearrange("p (m dk t) -> p m dk t", dk=2, t=5)
+            nc.vector.tensor_tensor(out=pl_t[e % 2][:, side, 0:UB * 25].rearrange("p (m t) -> p m t", t=5),
+                                    in0=hv[:, :, 0, :], in1=hv[:, :, 1, :], op=ALU.max)
+
+        def t_pl(e):
+            if not ok(e):
+                return
+            plT = pone.tile([P, 2, P], F32, name="plT", tag="e1")
             for side in range(2):
-                nc.tensor.transpose(plT[:, side, :], pl[:, side, :], ident_f[:])
+                nc.tensor.transpose(plT[:, side, :], pl_t[e % 2][:, side, :], ident_f[:])
+            live[("plT", e)] = plT
+
+        def cp_vals(e):
+            if not ok(e):
+                return
             vals = work.tile([P, 2, POS], F32, name="vals")
-            nc.scalar.copy(out=vals[:], in_=plT[:, :, 0:POS])
-            nc.sync.dma_start(out=out_0[b0:b0 + UB].rearrange("b c i j -> (b c) (i j)"),
+            nc.scalar.copy(out=vals[:], in_=live[("plT", e)][:, :, 0:POS])
+            nc.sync.dma_start(out=out_0[e * UB:(e + 1) * UB].rearrange("b c i j -> (b c) (i j)"),
                               in_=vals[0:UB * 25, 0, :])
-            nc.sync.dma_start(out=out_1[b0:b0 + UB].rearrange("b c k l -> (b c) (k l)"),
+            nc.sync.dma_start(out=out_1[e * UB:(e + 1) * UB].rearrange("b c k l -> (b c) (k l)"),
                               in_=vals[0:UB * 25, 1, :])
+
+        with tc.manual_schedule():
+            for k in range(-3, NU + 3):
+                load(k + 3, PP)
+                load(k + 3, QQ)
+                mx(k - 1)
+                powr(k, QQ)
+                mult(k, PP, 0)
+                sq(k + 1, PP, 0)
+                cp_vals(k - 3)
+                mult(k, PP, 1)
+                tr(k + 1, PP, 3)
+                bcast(k, QQ)
+                sq(k + 1, PP, 1)
+                mask(k - 1)
+                stt(k - 2)
+                t_sa(k - 1)
+                tr(k + 1, QQ, 0)
+                sq(k + 1, PP, 2)
+                t_xa(k - 2)
+                mult(k, PP, 2)
+                tr(k + 1, QQ, 1)
+                sq(k + 1, PP, 3)
+                mult(k, PP, 3)
+                tr(k + 1, QQ, 2)
+                powr(k + 1, PP)
+                mins(k - 1)
+                cp_xb(k - 2)
+                sq(k + 1, QQ, 0)
+                quant(k, PP)
+                tr(k + 1, QQ, 3)
+                exps(k - 1)
+                bcast(k + 1, PP)
+                pool(k - 2, 0)
+                mult(k, QQ, 0)
+                mult(k, QQ, 1)
+                sq(k + 1, QQ, 1)
+                recip(k - 1)
+                f2s(k - 1)
+                tr(k + 2, PP, 0)
+                mult(k, QQ, 2)
+                sq(k + 1, QQ, 2)
+                tr(k + 2, PP, 1)
+                mult(k, QQ, 3)
+                t_f2(k - 1)
+                sq(k + 1, QQ, 3)
+                pool(k - 2, 1)
+                t_pl(k - 2)
+                tr(k + 2, PP, 2)
+                quant(k, QQ)

@@ -36,8 +36,6 @@ def tile_corr_t_kernel(tc, xp, xq, alpha, out_0, out_1, out_2, out_3):
             tc.tile_pool(name="small", bufs=4) as small, \
             tc.psum_pool(name="pxt", bufs=3) as pxt, \
             tc.psum_pool(name="pone", bufs=1) as pone:
-        ident_b = const.tile([P, P], BF16, name="ident_b")
-        make_identity(nc, ident_b[:])
         ident_f = const.tile([P, P], F32, name="ident_f")
         make_identity(nc, ident_f[:])
         neg_half = const.tile([P, UB], F32, name="neg_half")
@@ -45,7 +43,7 @@ def tile_corr_t_kernel(tc, xp, xq, alpha, out_0, out_1, out_2, out_3):
         wneg = const.tile([P, POS], F32, name="wneg")
         junk = const.tile([P, CH * P], BF16, name="junk")
 
-        xt = [[fixed.tile([P, XW + 32], BF16, name="x%d_%d" % (o, k)) for k in range(NXB)] for o in range(2)]
+        xt = [[fixed.tile([P, XW + 64], BF16, name="x%d_%d" % (o, k)) for k in range(NXB)] for o in range(2)]
         yt = [fixed.tile([P, UB, 2, P, 4], BF16, name="y%d" % o, align_bytes=64) for o in range(2)]
         sa_t = [fixed.tile([P, EW + PADW], F32, name="sa%d" % k) for k in range(2)]
         f2_t = [fixed.tile([P, EW + PADW], F32, name="f2%d" % k) for k in range(2)]
@@ -53,7 +51,7 @@ def tile_corr_t_kernel(tc, xp, xq, alpha, out_0, out_1, out_2, out_3):
         pl_t = [fixed.tile([P, 2, P], F32, name="pl%d" % k) for k in range(2)]
         for o in range(2):
             for k in range(NXB):
-                nc.vector.memset(xt[o][k][:, XW:XW + 32], 0.0)
+                nc.vector.memset(xt[o][k][:, XW:XW + 64], 0.0)
             nc.vector.memset(yt[o][:, :, :, POS:P, :], 0.0)
         for k in range(2):
             nc.gpsimd.memset(sa_t[k][:, EW:EW + PADW], 0.0)
@@ -104,6 +102,25 @@ def tile_corr_t_kernel(tc, xp, xq, alpha, out_0, out_1, out_2, out_3):
         nc.vector.tensor_scalar(out=wneg[:], in0=wm1[:], scalar1=a_f[:, 0:1], scalar2=None, op0=ALU.mult)
 
 
+        posi = const.tile([P, P], I32, name="posi")
+        nc.gpsimd.iota(posi[:], pattern=[[1, P]], base=0, channel_multiplier=0)
+        posf = const.tile([P, P], F32, name="posf")
+        nc.vector.tensor_copy(out=posf[:], in_=posi[:])
+        s50 = const.tile([P, 1], F32, name="s50")
+        nc.vector.tensor_scalar(out=s50[:], in0=pf[:], scalar1=50.0, scalar2=-100.0, op0=ALU.is_ge, op1=ALU.mult)
+        s100 = const.tile([P, 1], F32, name="s100")
+        nc.vector.tensor_scalar(out=s100[:], in0=pf[:], scalar1=100.0, scalar2=-1000.0, op0=ALU.is_ge,
+                                op1=ALU.mult)
+        rv0 = const.tile([P, 1], F32, name="rv0")
+        nc.vector.scalar_tensor_tensor(out=rv0[:], in0=pf[:], scalar=2.0, in1=s50[:], op0=ALU.mult, op1=ALU.add)
+        rv = const.tile([P, 2], F32, name="rv")
+        nc.vector.tensor_tensor(out=rv[:, 0:1], in0=rv0[:], in1=s100[:], op=ALU.add)
+        nc.vector.tensor_scalar(out=rv[:, 1:2], in0=rv[:, 0:1], scalar1=1.0, scalar2=None, op0=ALU.add)
+        sel = [const.tile([P, P], F32, name="sel%d" % e) for e in range(2)]
+        for e in range(2):
+            nc.vector.tensor_scalar(out=sel[e][:], in0=posf[:], scalar1=rv[:, e:e + 1], scalar2=None,
+                                    op0=ALU.is_equal)
+
         live = {}
 
         def ok(k):
@@ -125,26 +142,45 @@ def tile_corr_t_kernel(tc, xp, xq, alpha, out_0, out_1, out_2, out_3):
             if not ok(k):
                 return
             x = xt[o][k % NXB]
-            xT = pxt.tile([P, CH * P], BF16, name="xT")
-            for t in range(CH):
-                c0 = (i * CH + t) * POS
-                nc.tensor.transpose(xT[:, t * P:(t + 1) * P], x[:, c0:c0 + P], ident_b[:])
+            xw = x[:].bitcast(F32)
+            xT = pxt.tile([P, 4 * P], F32, name="xT")
+            for v in range(4):
+                c0 = i * (CH * POS // 2) + v * POS
+                nc.tensor.transpose(xT[:, v * P:(v + 1) * P], xw[:, c0:c0 + P], ident_f[:])
             live[("xT", k, o, i)] = xT
 
         def sq(k, o, i):
             if not ok(k):
                 return
             if i == 0:
-                n2 = small.tile([P, UB], F32, name="n2")
-                live[("n2", k, o)] = n2
-            nc.scalar.activation(out=junk[:], in_=live[("xT", k, o, i)][:], func=ACT.Square,
-                                 accum_out=live[("n2", k, o)][:, i:i + 1])
+                acc = small.tile([P, 2 * UB], F32, name="acc")
+                live[("acc", k, o)] = acc
+            halves = live[("xT", k, o, i)][:].bitcast(BF16).rearrange("p (n e) -> p n e", e=2)
+            for e in range(2):
+                nc.scalar.activation(out=junk[:, 0:4 * P], in_=halves[:, :, e], func=ACT.Square,
+                                     accum_out=live[("acc", k, o)][:, e * UB + i:e * UB + i + 1])
+
+        def selmm(k, o):
+            if not ok(k):
+                return
+            n2p = pone.tile([P, UB], F32, name="n2p", tag="e2" if o == PP else "e0")
+            acc = live[("acc", k, o)]
+            for e in range(2):
+                nc.tensor.matmul(out=n2p[:], lhsT=sel[e][:], rhs=acc[:, e * UB:(e + 1) * UB],
+                                 start=(e == 0), stop=(e == 1))
+            live[("n2p", k, o)] = n2p
+
+        def evac(k, o):
+            if not ok(k):
+                return
+            n2c = small.tile([P, UB], F32, name="n2c")
+            nc.vector.tensor_scalar_max(out=n2c[:], in0=live[("n2p", k, o)][:], scalar1=EPS2)
+            live[("n2c", k, o)] = n2c
 
         def powr(k, o):
             if not ok(k):
                 return
-            n2c = small.tile([P, UB], F32, name="n2c")
-            nc.gpsimd.tensor_scalar_max(out=n2c[:], in0=live[("n2", k, o)][:], scalar1=EPS2)
+            n2c = live[("n2c", k, o)]
             rn = small.tile([P, UB], F32, name="rn")
             nc.gpsimd.tensor_tensor(out=rn[:], in0=n2c[:], in1=neg_half[:], op=ALU.pow)
             live[("rn", k, o)] = rn
@@ -341,8 +377,10 @@ def tile_corr_t_kernel(tc, xp, xq, alpha, out_0, out_1, out_2, out_3):
                 sq(k + 1, PP, 3)
                 mult(k, PP, 3)
                 tr(k + 1, QQ, 2)
-                powr(k + 1, PP)
+                selmm(k + 1, PP)
                 mins(k - 1)
+                evac(k + 1, PP)
+                powr(k + 1, PP)
                 cp_xb(k - 2)
                 sq(k + 1, QQ, 0)
                 quant(k, PP)
@@ -365,4 +403,6 @@ def tile_corr_t_kernel(tc, xp, xq, alpha, out_0, out_1, out_2, out_3):
                 pool(k - 2, 1)
                 t_pl(k - 2)
                 tr(k + 2, PP, 2)
+                selmm(k + 1, QQ)
                 quant(k, QQ)
+                evac(k + 1, QQ)

@@ -22,6 +22,7 @@ CH = 8
 XW = UB * CH * POS
 PADW = P - POS
 EW = UB * POS
+NSQ = 3
 NXB = 4
 EPS2 = 1e-24
 PP = 0
@@ -34,16 +35,19 @@ def tile_corr_t_kernel(tc, xp, xq, alpha, out_0, out_1, out_2, out_3):
             tc.tile_pool(name="fixed", bufs=1) as fixed, \
             tc.tile_pool(name="work", bufs=2) as work, \
             tc.tile_pool(name="small", bufs=4) as small, \
-            tc.psum_pool(name="pxt", bufs=3) as pxt, \
             tc.psum_pool(name="pone", bufs=1) as pone:
         ident_f = const.tile([P, P], F32, name="ident_f")
         make_identity(nc, ident_f[:])
         neg_half = const.tile([P, UB], F32, name="neg_half")
         nc.gpsimd.memset(neg_half[:], -0.5)
         wneg = const.tile([P, POS], F32, name="wneg")
-        junk = const.tile([P, CH * P], BF16, name="junk")
+        ones = const.tile([P, 2], F32, name="ones")
+        nc.gpsimd.memset(ones[:], 1.0)
+        sqt = [fixed.tile([P, CH * POS + PADW], F32, name="sq%d" % k) for k in range(NSQ)]
+        for k in range(NSQ):
+            nc.gpsimd.memset(sqt[k][:, CH * POS:CH * POS + PADW], 0.0)
 
-        xt = [[fixed.tile([P, XW + 64], BF16, name="x%d_%d" % (o, k)) for k in range(NXB)] for o in range(2)]
+        xt = [[fixed.tile([P, XW + 32], BF16, name="x%d_%d" % (o, k)) for k in range(NXB)] for o in range(2)]
         yt = [fixed.tile([P, UB, 2, P, 4], BF16, name="y%d" % o, align_bytes=64) for o in range(2)]
         sa_t = [fixed.tile([P, EW + PADW], F32, name="sa%d" % k) for k in range(2)]
         f2_t = [fixed.tile([P, EW + PADW], F32, name="f2%d" % k) for k in range(2)]
@@ -51,7 +55,7 @@ def tile_corr_t_kernel(tc, xp, xq, alpha, out_0, out_1, out_2, out_3):
         pl_t = [fixed.tile([P, 2, P], F32, name="pl%d" % k) for k in range(2)]
         for o in range(2):
             for k in range(NXB):
-                nc.vector.memset(xt[o][k][:, XW:XW + 64], 0.0)
+                nc.vector.memset(xt[o][k][:, XW:XW + 32], 0.0)
             nc.vector.memset(yt[o][:, :, :, POS:P, :], 0.0)
         for k in range(2):
             nc.gpsimd.memset(sa_t[k][:, EW:EW + PADW], 0.0)
@@ -102,25 +106,6 @@ def tile_corr_t_kernel(tc, xp, xq, alpha, out_0, out_1, out_2, out_3):
         nc.vector.tensor_scalar(out=wneg[:], in0=wm1[:], scalar1=a_f[:, 0:1], scalar2=None, op0=ALU.mult)
 
 
-        posi = const.tile([P, P], I32, name="posi")
-        nc.gpsimd.iota(posi[:], pattern=[[1, P]], base=0, channel_multiplier=0)
-        posf = const.tile([P, P], F32, name="posf")
-        nc.vector.tensor_copy(out=posf[:], in_=posi[:])
-        s50 = const.tile([P, 1], F32, name="s50")
-        nc.vector.tensor_scalar(out=s50[:], in0=pf[:], scalar1=50.0, scalar2=-100.0, op0=ALU.is_ge, op1=ALU.mult)
-        s100 = const.tile([P, 1], F32, name="s100")
-        nc.vector.tensor_scalar(out=s100[:], in0=pf[:], scalar1=100.0, scalar2=-1000.0, op0=ALU.is_ge,
-                                op1=ALU.mult)
-        rv0 = const.tile([P, 1], F32, name="rv0")
-        nc.vector.scalar_tensor_tensor(out=rv0[:], in0=pf[:], scalar=2.0, in1=s50[:], op0=ALU.mult, op1=ALU.add)
-        rv = const.tile([P, 2], F32, name="rv")
-        nc.vector.tensor_tensor(out=rv[:, 0:1], in0=rv0[:], in1=s100[:], op=ALU.add)
-        nc.vector.tensor_scalar(out=rv[:, 1:2], in0=rv[:, 0:1], scalar1=1.0, scalar2=None, op0=ALU.add)
-        sel = [const.tile([P, P], F32, name="sel%d" % e) for e in range(2)]
-        for e in range(2):
-            nc.vector.tensor_scalar(out=sel[e][:], in0=posf[:], scalar1=rv[:, e:e + 1], scalar2=None,
-                                    op0=ALU.is_equal)
-
         live = {}
 
         def ok(k):
@@ -138,52 +123,58 @@ def tile_corr_t_kernel(tc, xp, xq, alpha, out_0, out_1, out_2, out_3):
                 in_=src[k * UB:(k + 1) * UB].rearrange("b (g p j) h w -> p (b g) (j h w)", g=2, p=P, j=4),
             )
 
-        def tr(k, o, i):
-            if not ok(k):
-                return
-            x = xt[o][k % NXB]
-            xw = x[:].bitcast(F32)
-            xT = pxt.tile([P, 4 * P], F32, name="xT")
-            for v in range(4):
-                c0 = i * (CH * POS // 2) + v * POS
-                nc.tensor.transpose(xT[:, v * P:(v + 1) * P], xw[:, c0:c0 + P], ident_f[:])
-            live[("xT", k, o, i)] = xT
-
         def sq(k, o, i):
             if not ok(k):
                 return
-            if i == 0:
-                acc = small.tile([P, 2 * UB], F32, name="acc")
-                live[("acc", k, o)] = acc
-            halves = live[("xT", k, o, i)][:].bitcast(BF16).rearrange("p (n e) -> p n e", e=2)
-            for e in range(2):
-                nc.scalar.activation(out=junk[:, 0:4 * P], in_=halves[:, :, e], func=ACT.Square,
-                                     accum_out=live[("acc", k, o)][:, e * UB + i:e * UB + i + 1])
+            x = xt[o][k % NXB]
+            nc.scalar.activation(out=sqt[((k * 2 + o) * UB + i) % NSQ][:, 0:CH * POS],
+                                 in_=x[:, i * CH * POS:(i + 1) * CH * POS], func=ACT.Square)
 
-        def selmm(k, o):
+        def mm(k, o, i):
             if not ok(k):
                 return
-            n2p = pone.tile([P, UB], F32, name="n2p", tag="e2" if o == PP else "e0")
-            acc = live[("acc", k, o)]
-            for e in range(2):
-                nc.tensor.matmul(out=n2p[:], lhsT=sel[e][:], rhs=acc[:, e * UB:(e + 1) * UB],
-                                 start=(e == 0), stop=(e == 1))
-            live[("n2p", k, o)] = n2p
+            if i == 0:
+                n2p = pone.tile([P, UB, 2], F32, name="n2p", tag="n%d" % o)
+                live[("n2p", k, o)] = n2p
+            s = sqt[((k * 2 + o) * UB + i) % NSQ]
+            for t in range(CH):
+                nc.tensor.matmul(out=live[("n2p", k, o)][:, i, :], lhsT=s[:, t * POS:t * POS + P], rhs=ones[:],
+                                 start=(t == 0), stop=(t == CH - 1))
 
         def evac(k, o):
             if not ok(k):
                 return
             n2c = small.tile([P, UB], F32, name="n2c")
-            nc.vector.tensor_scalar_max(out=n2c[:], in0=live[("n2p", k, o)][:], scalar1=EPS2)
+            nc.vector.tensor_scalar_max(out=n2c[:], in0=live[("n2p", k, o)][:, :, 0], scalar1=EPS2)
             live[("n2c", k, o)] = n2c
 
         def powr(k, o):
             if not ok(k):
                 return
-            n2c = live[("n2c", k, o)]
             rn = small.tile([P, UB], F32, name="rn")
-            nc.gpsimd.tensor_tensor(out=rn[:], in0=n2c[:], in1=neg_half[:], op=ALU.pow)
+            nc.gpsimd.tensor_tensor(out=rn[:], in0=live[("n2c", k, o)][:], in1=neg_half[:], op=ALU.pow)
             live[("rn", k, o)] = rn
+
+        def rbs(k, o):
+            if not ok(k):
+                return
+            rc = work.tile([P, POS], F32, name="rc", tag="rc%d" % o)
+            nc.scalar.copy(out=rc[:], in_=live[("rb", k, o)][:, UB - 1, 0:POS])
+            live[("rc", k, o)] = rc
+
+        def gmult(k, o):
+            if not ok(k):
+                return
+            x = xt[o][k % NXB]
+            i = UB - 1
+            for g in range(2):
+                c0 = (i * 2 + g) * 4 * POS
+                nc.gpsimd.tensor_tensor(
+                    out=yt[o][:, i, g, 0:POS, :],
+                    in0=x[:, c0:c0 + 4 * POS].rearrange("p (j w) -> p w j", j=4),
+                    in1=live[("rc", k, o)][:].unsqueeze(2).to_broadcast([P, POS, 4]),
+                    op=ALU.mult,
+                )
 
         def bcast(k, o):
             if not ok(k):
@@ -288,10 +279,9 @@ def tile_corr_t_kernel(tc, xp, xq, alpha, out_0, out_1, out_2, out_3):
             rs = live[("rs", e)]
             e2 = live[("e2", e)]
             for i in range(UB):
-                nc.gpsimd.tensor_scalar(out=f2_t[e % 2][:, i * POS:(i + 1) * POS],
-                                        in0=e2[:, i * POS:(i + 1) * POS],
-                                        scalar1=rs[:, UB + i:UB + i + 1], scalar2=1.0,
-                                        op0=ALU.mult, op1=ALU.mult)
+                nc.scalar.activation(out=f2_t[e % 2][:, i * POS:(i + 1) * POS],
+                                     in_=e2[:, i * POS:(i + 1) * POS], func=ACT.Copy,
+                                     scale=rs[:, UB + i:UB + i + 1])
 
         def t_f2(e):
             if ok(e):
@@ -361,48 +351,48 @@ def tile_corr_t_kernel(tc, xp, xq, alpha, out_0, out_1, out_2, out_3):
                 powr(k, QQ)
                 mult(k, PP, 0)
                 sq(k + 1, PP, 0)
+                mm(k + 1, PP, 0)
                 cp_vals(k - 3)
                 mult(k, PP, 1)
-                tr(k + 1, PP, 3)
                 bcast(k, QQ)
                 sq(k + 1, PP, 1)
+                mm(k + 1, PP, 1)
+                rbs(k, QQ)
+                gmult(k, QQ)
                 mask(k - 1)
                 stt(k - 2)
                 t_sa(k - 1)
-                tr(k + 1, QQ, 0)
                 sq(k + 1, PP, 2)
+                mm(k + 1, PP, 2)
                 t_xa(k - 2)
                 mult(k, PP, 2)
-                tr(k + 1, QQ, 1)
                 sq(k + 1, PP, 3)
-                mult(k, PP, 3)
-                tr(k + 1, QQ, 2)
-                selmm(k + 1, PP)
+                mm(k + 1, PP, 3)
+                cp_xb(k - 2)
                 mins(k - 1)
                 evac(k + 1, PP)
                 powr(k + 1, PP)
-                cp_xb(k - 2)
-                sq(k + 1, QQ, 0)
                 quant(k, PP)
-                tr(k + 1, QQ, 3)
+                sq(k + 1, QQ, 0)
+                mm(k + 1, QQ, 0)
                 exps(k - 1)
                 bcast(k + 1, PP)
                 pool(k - 2, 0)
+                rbs(k + 1, PP)
+                gmult(k + 1, PP)
                 mult(k, QQ, 0)
                 mult(k, QQ, 1)
                 sq(k + 1, QQ, 1)
+                mm(k + 1, QQ, 1)
                 recip(k - 1)
-                f2s(k - 1)
-                tr(k + 2, PP, 0)
                 mult(k, QQ, 2)
                 sq(k + 1, QQ, 2)
-                tr(k + 2, PP, 1)
-                mult(k, QQ, 3)
-                t_f2(k - 1)
-                sq(k + 1, QQ, 3)
+                mm(k + 1, QQ, 2)
                 pool(k - 2, 1)
                 t_pl(k - 2)
-                tr(k + 2, PP, 2)
-                selmm(k + 1, QQ)
+                sq(k + 1, QQ, 3)
+                mm(k + 1, QQ, 3)
+                f2s(k - 1)
+                t_f2(k - 1)
                 quant(k, QQ)
                 evac(k + 1, QQ)

@@ -22,7 +22,6 @@ CH = 8
 XW = UB * CH * POS
 PADW = P - POS
 EW = UB * POS
-NSQ = 3
 NXB = 4
 EPS2 = 1e-24
 PP = 0
@@ -35,17 +34,16 @@ def tile_corr_t_kernel(tc, xp, xq, alpha, out_0, out_1, out_2, out_3):
             tc.tile_pool(name="fixed", bufs=1) as fixed, \
             tc.tile_pool(name="work", bufs=2) as work, \
             tc.tile_pool(name="small", bufs=4) as small, \
+            tc.psum_pool(name="pxt", bufs=3) as pxt, \
             tc.psum_pool(name="pone", bufs=1) as pone:
+        ident_b = const.tile([P, P], BF16, name="ident_b")
+        make_identity(nc, ident_b[:])
         ident_f = const.tile([P, P], F32, name="ident_f")
         make_identity(nc, ident_f[:])
         neg_half = const.tile([P, UB], F32, name="neg_half")
         nc.gpsimd.memset(neg_half[:], -0.5)
         wneg = const.tile([P, POS], F32, name="wneg")
-        ones = const.tile([P, 2], F32, name="ones")
-        nc.gpsimd.memset(ones[:], 1.0)
-        sqt = [fixed.tile([P, CH * POS + PADW], F32, name="sq%d" % k) for k in range(NSQ)]
-        for k in range(NSQ):
-            nc.gpsimd.memset(sqt[k][:, CH * POS:CH * POS + PADW], 0.0)
+        junk = const.tile([P, CH * P], BF16, name="junk")
 
         xt = [[fixed.tile([P, XW + 32], BF16, name="x%d_%d" % (o, k)) for k in range(NXB)] for o in range(2)]
         yt = [fixed.tile([P, UB, 2, P, 4], BF16, name="y%d" % o, align_bytes=64) for o in range(2)]
@@ -118,48 +116,65 @@ def tile_corr_t_kernel(tc, xp, xq, alpha, out_0, out_1, out_2, out_3):
             if not ok(k):
                 return
             src = xp if o == PP else xq
-            nc.sync.dma_start(
-                out=xt[o][k % NXB][:, 0:XW].rearrange("p (n f) -> p n f", n=2 * UB),
-                in_=src[k * UB:(k + 1) * UB].rearrange("b (g p j) h w -> p (b g) (j h w)", g=2, p=P, j=4),
-            )
+            step = 1 if k == 0 else UB
+            for i in range(0, UB, step):
+                nc.sync.dma_start(
+                    out=xt[o][k % NXB][:, i * CH * POS:(i + step) * CH * POS].rearrange(
+                        "p (n f) -> p n f", n=2 * step),
+                    in_=src[k * UB + i:k * UB + i + step].rearrange(
+                        "b (g p j) h w -> p (b g) (j h w)", g=2, p=P, j=4),
+                )
+
+        def tr(k, o, i):
+            if not ok(k):
+                return
+            x = xt[o][k % NXB]
+            xT = pxt.tile([P, CH * P], BF16, name="xT")
+            for t in range(CH):
+                c0 = (i * CH + t) * POS
+                nc.tensor.transpose(xT[:, t * P:(t + 1) * P], x[:, c0:c0 + P], ident_b[:])
+            live[("xT", k, o, i)] = xT
 
         def sq(k, o, i):
             if not ok(k):
                 return
-            x = xt[o][k % NXB]
-            nc.scalar.activation(out=sqt[((k * 2 + o) * UB + i) % NSQ][:, 0:CH * POS],
-                                 in_=x[:, i * CH * POS:(i + 1) * CH * POS], func=ACT.Square)
-
-        def mm(k, o, i):
-            if not ok(k):
-                return
             if i == 0:
-                n2p = pone.tile([P, UB, 2], F32, name="n2p", tag="n%d" % o)
-                live[("n2p", k, o)] = n2p
-            s = sqt[((k * 2 + o) * UB + i) % NSQ]
-            for t in range(CH):
-                nc.tensor.matmul(out=live[("n2p", k, o)][:, i, :], lhsT=s[:, t * POS:t * POS + P], rhs=ones[:],
-                                 start=(t == 0), stop=(t == CH - 1))
+                n2 = small.tile([P, UB], F32, name="n2")
+                live[("n2", k, o)] = n2
+            nc.scalar.activation(out=junk[:], in_=live[("xT", k, o, i)][:], func=ACT.Square,
+                                 accum_out=live[("n2", k, o)][:, i:i + 1])
+            if k == 0:
+                norm(k, o, i, i + 1)
+                spread(k, o, i, i + 1)
 
-        def evac(k, o):
-            if not ok(k):
-                return
-            n2c = small.tile([P, UB], F32, name="n2c")
-            nc.vector.tensor_scalar_max(out=n2c[:], in0=live[("n2p", k, o)][:, :, 0], scalar1=EPS2)
-            live[("n2c", k, o)] = n2c
+        def norm(k, o, lo, hi):
+            if lo == 0:
+                n2c = small.tile([P, UB], F32, name="n2c")
+                rn = small.tile([P, UB], F32, name="rn")
+                live[("n2c", k, o)] = n2c
+                live[("rn", k, o)] = rn
+            nc.gpsimd.tensor_scalar_max(out=live[("n2c", k, o)][:, lo:hi], in0=live[("n2", k, o)][:, lo:hi],
+                                        scalar1=EPS2)
+            nc.gpsimd.tensor_tensor(out=live[("rn", k, o)][:, lo:hi], in0=live[("n2c", k, o)][:, lo:hi],
+                                    in1=neg_half[:, lo:hi], op=ALU.pow)
+
+        def spread(k, o, lo, hi):
+            if lo == 0:
+                rb = pone.tile([P, UB, P], F32, name="rb", tag="rb%d" % o)
+                live[("rb", k, o)] = rb
+            for i in range(lo, hi):
+                nc.tensor.transpose(live[("rb", k, o)][:, i, :],
+                                    live[("rn", k, o)][:, i:i + 1].to_broadcast([P, P]), ident_f[:])
 
         def powr(k, o):
-            if not ok(k):
-                return
-            rn = small.tile([P, UB], F32, name="rn")
-            nc.gpsimd.tensor_tensor(out=rn[:], in0=live[("n2c", k, o)][:], in1=neg_half[:], op=ALU.pow)
-            live[("rn", k, o)] = rn
+            if 0 < k < NU:
+                norm(k, o, 0, UB)
 
         def rbs(k, o):
             if not ok(k):
                 return
             rc = work.tile([P, POS], F32, name="rc", tag="rc%d" % o)
-            nc.scalar.copy(out=rc[:], in_=live[("rb", k, o)][:, UB - 1, 0:POS])
+            nc.vector.tensor_copy(out=rc[:], in_=live[("rb", k, o)][:, UB - 1, 0:POS])
             live[("rc", k, o)] = rc
 
         def gmult(k, o):
@@ -177,13 +192,8 @@ def tile_corr_t_kernel(tc, xp, xq, alpha, out_0, out_1, out_2, out_3):
                 )
 
         def bcast(k, o):
-            if not ok(k):
-                return
-            rb = pone.tile([P, UB, P], F32, name="rb", tag="rb%d" % o)
-            rn = live[("rn", k, o)]
-            for i in range(UB):
-                nc.tensor.transpose(rb[:, i, :], rn[:, i:i + 1].to_broadcast([P, P]), ident_f[:])
-            live[("rb", k, o)] = rb
+            if 0 < k < NU:
+                spread(k, o, 0, UB)
 
         def mult(k, o, i):
             if not ok(k):
@@ -309,7 +319,7 @@ def tile_corr_t_kernel(tc, xp, xq, alpha, out_0, out_1, out_2, out_3):
             if not ok(e):
                 return
             xb = work.tile([P, EW], F32, name="xb")
-            nc.scalar.copy(out=img(xb[:]), in_=live[("xbT", e)][:, :, 0:POS])
+            nc.vector.tensor_copy(out=img(xb[:]), in_=live[("xbT", e)][:, :, 0:POS])
             nc.sync.dma_start(out=out_2[e * UB:(e + 1) * UB].rearrange("b q i j -> q b (i j)"),
                               in_=img(xb[0:POS, :]))
             live[("xb", e)] = xb
@@ -337,7 +347,7 @@ def tile_corr_t_kernel(tc, xp, xq, alpha, out_0, out_1, out_2, out_3):
             if not ok(e):
                 return
             vals = work.tile([P, 2, POS], F32, name="vals")
-            nc.scalar.copy(out=vals[:], in_=live[("plT", e)][:, :, 0:POS])
+            nc.vector.tensor_copy(out=vals[:], in_=live[("plT", e)][:, :, 0:POS])
             nc.sync.dma_start(out=out_0[e * UB:(e + 1) * UB].rearrange("b c i j -> (b c) (i j)"),
                               in_=vals[0:UB * 25, 0, :])
             nc.sync.dma_start(out=out_1[e * UB:(e + 1) * UB].rearrange("b c k l -> (b c) (k l)"),
@@ -349,50 +359,48 @@ def tile_corr_t_kernel(tc, xp, xq, alpha, out_0, out_1, out_2, out_3):
                 load(k + 3, QQ)
                 mx(k - 1)
                 powr(k, QQ)
+                gmult(k, PP)
                 mult(k, PP, 0)
                 sq(k + 1, PP, 0)
-                mm(k + 1, PP, 0)
                 cp_vals(k - 3)
                 mult(k, PP, 1)
+                tr(k + 1, PP, 3)
                 bcast(k, QQ)
                 sq(k + 1, PP, 1)
-                mm(k + 1, PP, 1)
-                rbs(k, QQ)
-                gmult(k, QQ)
                 mask(k - 1)
                 stt(k - 2)
                 t_sa(k - 1)
+                tr(k + 1, QQ, 0)
                 sq(k + 1, PP, 2)
-                mm(k + 1, PP, 2)
                 t_xa(k - 2)
                 mult(k, PP, 2)
+                tr(k + 1, QQ, 1)
                 sq(k + 1, PP, 3)
-                mm(k + 1, PP, 3)
-                cp_xb(k - 2)
-                mins(k - 1)
-                evac(k + 1, PP)
+                tr(k + 1, QQ, 2)
                 powr(k + 1, PP)
-                quant(k, PP)
+                mins(k - 1)
+                cp_xb(k - 2)
                 sq(k + 1, QQ, 0)
-                mm(k + 1, QQ, 0)
+                quant(k, PP)
+                rbs(k, QQ)
+                gmult(k, QQ)
+                tr(k + 1, QQ, 3)
                 exps(k - 1)
                 bcast(k + 1, PP)
                 pool(k - 2, 0)
-                rbs(k + 1, PP)
-                gmult(k + 1, PP)
                 mult(k, QQ, 0)
                 mult(k, QQ, 1)
                 sq(k + 1, QQ, 1)
-                mm(k + 1, QQ, 1)
                 recip(k - 1)
+                tr(k + 2, PP, 0)
                 mult(k, QQ, 2)
+                rbs(k + 1, PP)
                 sq(k + 1, QQ, 2)
-                mm(k + 1, QQ, 2)
-                pool(k - 2, 1)
-                t_pl(k - 2)
+                tr(k + 2, PP, 1)
                 sq(k + 1, QQ, 3)
-                mm(k + 1, QQ, 3)
                 f2s(k - 1)
                 t_f2(k - 1)
+                pool(k - 2, 1)
+                t_pl(k - 2)
+                tr(k + 2, PP, 2)
                 quant(k, QQ)
-                evac(k + 1, QQ)

@@ -199,12 +199,15 @@ def tile_corr_t_kernel(tc, xp, xq, alpha, out_0, out_1, out_2, out_3):
             if not ok(k):
                 return
             x = xt[o][k % NXB]
-            nc.vector.tensor_tensor(
-                out=yt[o][:, i, :, 0:POS, :],
-                in0=x[:, i * CH * POS:(i + 1) * CH * POS].rearrange("p (g j w) -> p g w j", g=2, j=4),
-                in1=live[("rb", k, o)][:, i, 0:POS].unsqueeze(1).unsqueeze(3).to_broadcast([P, 2, POS, 4]),
-                op=ALU.mult,
-            )
+            for g in range(2):
+                c0 = (i * 2 + g) * 4 * POS
+                nc.vector.tensor_tensor(
+                    out=yt[o][:, i, g, 0:POS, :].rearrange("p (c n) j -> p c j n", n=4),
+                    in0=x[:, c0:c0 + 4 * POS].rearrange("p (j c n) -> p c j n", j=4, n=4),
+                    in1=live[("rb", k, o)][:, i, 0:POS].rearrange("p (c n) -> p c n", n=4).unsqueeze(2).to_broadcast(
+                        [P, POS // 4, 4, 4]),
+                    op=ALU.mult,
+                )
 
         def quant(k, o):
             if not ok(k):

@@ -331,12 +331,10 @@ def tile_corr_t_kernel(tc, xp, xq, alpha, out_0, out_1, out_2, out_3):
             if not ok(e):
                 return
             srcx = xa_t[e % 2] if side == 0 else live[("xb", e)]
-            pair = srcx[:, 0:EW].rearrange("p (n two) -> p n two", two=2)
-            hm = work.tile([P, EW // 2], F32, name="hm")
-            nc.vector.tensor_tensor(out=hm[:], in0=pair[:, :, 0], in1=pair[:, :, 1], op=ALU.max)
-            hv = hm[:].rearrange("p (m dk t) -> p m dk t", dk=2, t=5)
-            nc.vector.tensor_tensor(out=pl_t[e % 2][:, side, 0:UB * 25].rearrange("p (m t) -> p m t", t=5),
-                                    in0=hv[:, :, 0, :], in1=hv[:, :, 1, :], op=ALU.max)
+            nc.vector.tensor_reduce(
+                out=pl_t[e % 2][:, side, 0:UB * 25].rearrange("p (m t) -> p m t", t=5),
+                in_=srcx[:, 0:EW].rearrange("p (m dk t dl) -> p m t dk dl", dk=2, t=5, dl=2),
+                axis=AX.XY, op=ALU.max)
 
         def t_pl(e):
             if not ok(e):
@@ -397,7 +395,6 @@ def tile_corr_t_kernel(tc, xp, xq, alpha, out_0, out_1, out_2, out_3):
                 recip(k - 1)
                 tr(k + 2, PP, 0)
                 mult(k, QQ, 2)
-                rbs(k + 1, PP)
                 sq(k + 1, QQ, 2)
                 tr(k + 2, PP, 1)
                 sq(k + 1, QQ, 3)
@@ -407,3 +404,4 @@ def tile_corr_t_kernel(tc, xp, xq, alpha, out_0, out_1, out_2, out_3):
                 t_pl(k - 2)
                 tr(k + 2, PP, 2)
                 quant(k, QQ)
+                rbs(k + 1, PP)

@@ -173,21 +173,20 @@ def tile_corr_t_kernel(tc, xp, xq, alpha, out_0, out_1, out_2, out_3):
         def rbs(k, o):
             if not ok(k):
                 return
-            rc = work.tile([P, POS], F32, name="rc", tag="rc%d" % o)
-            nc.vector.tensor_copy(out=rc[:], in_=live[("rb", k, o)][:, UB - 1, 0:POS])
+            rc = work.tile([P, 2, POS], F32, name="rc", tag="rc%d" % o)
+            nc.vector.tensor_copy(out=rc[:], in_=live[("rb", k, o)][:, UB - 2:UB, 0:POS])
             live[("rc", k, o)] = rc
 
         def gmult(k, o):
             if not ok(k):
                 return
             x = xt[o][k % NXB]
-            i = UB - 1
-            for g in range(2):
+            for i, g in ((UB - 1, 0), (UB - 1, 1), (UB - 2, 1)):
                 c0 = (i * 2 + g) * 4 * POS
                 nc.gpsimd.tensor_tensor(
                     out=yt[o][:, i, g, 0:POS, :],
                     in0=x[:, c0:c0 + 4 * POS].rearrange("p (j w) -> p w j", j=4),
-                    in1=live[("rc", k, o)][:].unsqueeze(2).to_broadcast([P, POS, 4]),
+                    in1=live[("rc", k, o)][:, i - UB + 2, :].unsqueeze(2).to_broadcast([P, POS, 4]),
                     op=ALU.mult,
                 )
 
@@ -199,7 +198,7 @@ def tile_corr_t_kernel(tc, xp, xq, alpha, out_0, out_1, out_2, out_3):
             if not ok(k):
                 return
             x = xt[o][k % NXB]
-            for g in range(2):
+            for g in range(1 if i == UB - 2 else 2):
                 c0 = (i * 2 + g) * 4 * POS
                 nc.vector.tensor_tensor(
                     out=yt[o][:, i, g, 0:POS, :].rearrange("p (c n) j -> p c j n", n=4),

@@ -42,6 +42,8 @@ def tile_corr_t_kernel(tc, xp, xq, alpha, out_0, out_1, out_2, out_3):
         make_identity(nc, ident_f[:])
         neg_half = const.tile([P, UB], F32, name="neg_half")
         nc.gpsimd.memset(neg_half[:], -0.5)
+        first = const.tile([P, 1], F32, name="first")
+        nc.scalar.activation(out=first[:], in_=neg_half[:, 0:1], func=ACT.Exp)
         wneg = const.tile([P, POS], F32, name="wneg")
         junk = const.tile([P, CH * P], BF16, name="junk")
 
@@ -89,20 +91,6 @@ def tile_corr_t_kernel(tc, xp, xq, alpha, out_0, out_1, out_2, out_3):
                                 op0=ALU.subtract)
         d2 = const.tile([P, 2, 10], F32, name="d2")
         nc.vector.tensor_tensor(out=d2[:], in0=dd[:], in1=dd[:], op=ALU.mult)
-        gg = const.tile([P, 2, 10], F32, name="gg")
-        nc.scalar.activation(out=gg[:], in_=d2[:], func=ACT.Exp, scale=-2.0)
-        g2 = const.tile([P, 10, 10], F32, name="g2")
-        nc.vector.tensor_tensor(out=g2[:],
-                                in0=gg[:, 0, :].unsqueeze(2).to_broadcast([P, 10, 10]),
-                                in1=gg[:, 1, :].unsqueeze(1).to_broadcast([P, 10, 10]),
-                                op=ALU.mult)
-        a_f = const.tile([P, 1], F32, name="a_f")
-        nc.vector.tensor_copy(out=a_f[:], in_=a_bf[:])
-        wm1 = const.tile([P, POS], F32, name="wm1")
-        nc.vector.tensor_scalar(out=wm1[:], in0=g2[:].rearrange("p k l -> p (k l)"), scalar1=1.0,
-                                scalar2=None, op0=ALU.subtract)
-        nc.vector.tensor_scalar(out=wneg[:], in0=wm1[:], scalar1=a_f[:, 0:1], scalar2=None, op0=ALU.mult)
-
 
         live = {}
 
@@ -181,12 +169,14 @@ def tile_corr_t_kernel(tc, xp, xq, alpha, out_0, out_1, out_2, out_3):
             if not ok(k):
                 return
             x = xt[o][k % NXB]
-            for i, g in ((UB - 1, 0), (UB - 1, 1), (UB - 2, 1)):
-                c0 = (i * 2 + g) * 4 * POS
+            for i, g0 in ((UB - 1, 0), (UB - 2, 1)):
+                ng = 2 - g0
+                c0 = (i * 2 + g0) * 4 * POS
                 nc.gpsimd.tensor_tensor(
-                    out=yt[o][:, i, g, 0:POS, :],
-                    in0=x[:, c0:c0 + 4 * POS].rearrange("p (j w) -> p w j", j=4),
-                    in1=live[("rc", k, o)][:, i - UB + 2, :].unsqueeze(2).to_broadcast([P, POS, 4]),
+                    out=yt[o][:, i, g0:2, 0:POS, :],
+                    in0=x[:, c0:c0 + ng * 4 * POS].rearrange("p (g j w) -> p g w j", g=ng, j=4),
+                    in1=live[("rc", k, o)][:, i - UB + 2, :].unsqueeze(1).unsqueeze(3).to_broadcast(
+                        [P, ng, POS, 4]),
                     op=ALU.mult,
                 )
 
@@ -290,10 +280,7 @@ def tile_corr_t_kernel(tc, xp, xq, alpha, out_0, out_1, out_2, out_3):
                 return
             rs = live[("rs", e)]
             e2 = live[("e2", e)]
-            for i in range(UB):
-                nc.scalar.activation(out=f2_t[e % 2][:, i * POS:(i + 1) * POS],
-                                     in_=e2[:, i * POS:(i + 1) * POS], func=ACT.Copy,
-                                     scale=rs[:, UB + i:UB + i + 1])
+            nc.vector.tensor_tensor(out=img(f2_t[e % 2][:, 0:EW]), in0=img(e2[:]), in1=rs[:, UB:2 * UB].unsqueeze(2).to_broadcast([P, UB, POS]), op=ALU.mult)
 
         def t_f2(e):
             if ok(e):
@@ -353,6 +340,21 @@ def tile_corr_t_kernel(tc, xp, xq, alpha, out_0, out_1, out_2, out_3):
             nc.sync.dma_start(out=out_1[e * UB:(e + 1) * UB].rearrange("b c k l -> (b c) (k l)"),
                               in_=vals[0:UB * 25, 1, :])
 
+        def window():
+            gg = const.tile([P, 2, 10], F32, name="gg")
+            nc.scalar.activation(out=gg[:], in_=d2[:], func=ACT.Exp, scale=-2.0)
+            g2 = const.tile([P, 10, 10], F32, name="g2")
+            nc.vector.tensor_tensor(out=g2[:],
+                                    in0=gg[:, 0, :].unsqueeze(2).to_broadcast([P, 10, 10]),
+                                    in1=gg[:, 1, :].unsqueeze(1).to_broadcast([P, 10, 10]),
+                                    op=ALU.mult)
+            a_f = const.tile([P, 1], F32, name="a_f")
+            nc.vector.tensor_copy(out=a_f[:], in_=a_bf[:])
+            wm1 = const.tile([P, POS], F32, name="wm1")
+            nc.vector.tensor_scalar(out=wm1[:], in0=g2[:].rearrange("p k l -> p (k l)"), scalar1=1.0,
+                                    scalar2=None, op0=ALU.subtract)
+            nc.vector.tensor_scalar(out=wneg[:], in0=wm1[:], scalar1=a_f[:, 0:1], scalar2=None, op0=ALU.mult)
+
         with tc.manual_schedule():
             for k in range(-3, NU + 3):
                 load(k + 3, PP)
@@ -374,20 +376,22 @@ def tile_corr_t_kernel(tc, xp, xq, alpha, out_0, out_1, out_2, out_3):
                 sq(k + 1, PP, 2)
                 t_xa(k - 2)
                 mult(k, PP, 2)
+                rbs(k, QQ)
                 tr(k + 1, QQ, 1)
                 sq(k + 1, PP, 3)
                 tr(k + 1, QQ, 2)
+                if k == -1:
+                    window()
                 powr(k + 1, PP)
                 mins(k - 1)
-                cp_xb(k - 2)
                 sq(k + 1, QQ, 0)
                 quant(k, PP)
-                rbs(k, QQ)
                 gmult(k, QQ)
                 tr(k + 1, QQ, 3)
                 exps(k - 1)
                 bcast(k + 1, PP)
                 pool(k - 2, 0)
+                cp_xb(k - 2)
                 mult(k, QQ, 0)
                 mult(k, QQ, 1)
                 sq(k + 1, QQ, 1)

@@ -100,6 +100,10 @@ def tile_corr_t_kernel(tc, xp, xq, alpha, out_0, out_1, out_2, out_3):
         def img(ap):
             return ap.rearrange("p (b q) -> p b q", b=UB)
 
+        def store(dst, src):
+            for lo, hi in ((0, 64), (64, 96), (96, 100)):
+                nc.sync.dma_start(out=dst[lo:hi], in_=src[lo:hi])
+
         def load(k, o):
             if not ok(k):
                 return
@@ -301,16 +305,14 @@ def tile_corr_t_kernel(tc, xp, xq, alpha, out_0, out_1, out_2, out_3):
             if not ok(e):
                 return
             turn(e, "xbT", xa_t[e % 2], "e0")
-            nc.sync.dma_start(out=out_3[e * UB:(e + 1) * UB].rearrange("b p k l -> p b (k l)"),
-                              in_=img(xa_t[e % 2][0:POS, 0:EW]))
+            store(out_3[e * UB:(e + 1) * UB].rearrange("b p k l -> p b (k l)"), img(xa_t[e % 2][0:POS, 0:EW]))
 
         def cp_xb(e):
             if not ok(e):
                 return
             xb = work.tile([P, EW], F32, name="xb")
             nc.vector.tensor_copy(out=img(xb[:]), in_=live[("xbT", e)][:, :, 0:POS])
-            nc.sync.dma_start(out=out_2[e * UB:(e + 1) * UB].rearrange("b q i j -> q b (i j)"),
-                              in_=img(xb[0:POS, :]))
+            store(out_2[e * UB:(e + 1) * UB].rearrange("b q i j -> q b (i j)"), img(xb[0:POS, :]))
             live[("xb", e)] = xb
 
         def pool(e, side):
@@ -335,10 +337,8 @@ def tile_corr_t_kernel(tc, xp, xq, alpha, out_0, out_1, out_2, out_3):
                 return
             vals = work.tile([P, 2, POS], F32, name="vals")
             nc.vector.tensor_copy(out=vals[:], in_=live[("plT", e)][:, :, 0:POS])
-            nc.sync.dma_start(out=out_0[e * UB:(e + 1) * UB].rearrange("b c i j -> (b c) (i j)"),
-                              in_=vals[0:UB * 25, 0, :])
-            nc.sync.dma_start(out=out_1[e * UB:(e + 1) * UB].rearrange("b c k l -> (b c) (k l)"),
-                              in_=vals[0:UB * 25, 1, :])
+            store(out_0[e * UB:(e + 1) * UB].rearrange("b c i j -> (b c) (i j)"), vals[0:UB * 25, 0, :])
+            store(out_1[e * UB:(e + 1) * UB].rearrange("b c k l -> (b c) (k l)"), vals[0:UB * 25, 1, :])
 
         def window():
             gg = const.tile([P, 2, 10], F32, name="gg")

@@ -22,6 +22,7 @@ CH = 8
 XW = UB * CH * POS
 PADW = P - POS
 EW = UB * POS
+BL = 25
 NXB = 4
 EPS2 = 1e-24
 PP = 0
@@ -50,8 +51,8 @@ def tile_corr_t_kernel(tc, xp, xq, alpha, out_0, out_1, out_2, out_3):
         xt = [[fixed.tile([P, XW + 32], BF16, name="x%d_%d" % (o, k)) for k in range(NXB)] for o in range(2)]
         yt = [fixed.tile([P, UB, 2, P, 4], BF16, name="y%d" % o, align_bytes=64) for o in range(2)]
         sa_t = [fixed.tile([P, EW + PADW], F32, name="sa%d" % k) for k in range(2)]
-        f2_t = [fixed.tile([P, EW + PADW], F32, name="f2%d" % k) for k in range(2)]
-        xa_t = [fixed.tile([P, EW + PADW], F32, name="xa%d" % k) for k in range(2)]
+        f2_t = [fixed.tile([P, UB, P], F32, name="f2%d" % k) for k in range(2)]
+        xa_t = [fixed.tile([P, UB, P], F32, name="xa%d" % k) for k in range(2)]
         pl_t = [fixed.tile([P, 2, P], F32, name="pl%d" % k) for k in range(2)]
         for o in range(2):
             for k in range(NXB):
@@ -59,8 +60,8 @@ def tile_corr_t_kernel(tc, xp, xq, alpha, out_0, out_1, out_2, out_3):
             nc.vector.memset(yt[o][:, :, :, POS:P, :], 0.0)
         for k in range(2):
             nc.gpsimd.memset(sa_t[k][:, EW:EW + PADW], 0.0)
-            nc.gpsimd.memset(f2_t[k][:, EW:EW + PADW], 0.0)
-            nc.gpsimd.memset(xa_t[k][:, EW:EW + PADW], 0.0)
+            nc.gpsimd.memset(f2_t[k][:, :, POS:P], 0.0)
+            nc.gpsimd.memset(xa_t[k][:, :, POS:P], 0.0)
             nc.gpsimd.memset(pl_t[k][:], 0.0)
 
         a_bf = const.tile([P, 1], BF16, name="a_bf")
@@ -103,6 +104,10 @@ def tile_corr_t_kernel(tc, xp, xq, alpha, out_0, out_1, out_2, out_3):
         def store(dst, src):
             for lo, hi in ((0, 64), (64, 96), (96, 100)):
                 nc.sync.dma_start(out=dst[lo:hi], in_=src[lo:hi])
+
+        def vals(dst, e, rows):
+            if ok(e):
+                nc.sync.dma_start(out=dst[e * UB:(e + 1) * UB].rearrange("b c i j -> c b (i j)"), in_=rows)
 
         def load(k, o):
             if not ok(k):
@@ -232,15 +237,15 @@ def tile_corr_t_kernel(tc, xp, xq, alpha, out_0, out_1, out_2, out_3):
             nc.vector.tensor_tensor(out=img(sa_t[e % 2][:, 0:EW]), in0=live[("aff", e)][:, :, 0:POS],
                                     in1=wneg[:].unsqueeze(1).to_broadcast([P, UB, POS]), op=ALU.mult)
 
-        def turn(e, key, src, tag):
+        def turn(e, key, windows, tag):
             dst = pone.tile([P, UB, P], F32, name=key, tag=tag)
             for i in range(UB):
-                nc.tensor.transpose(dst[:, i, :], src[:, i * POS:i * POS + P], ident_f[:])
+                nc.tensor.transpose(dst[:, i, :], windows[i], ident_f[:])
             live[(key, e)] = dst
 
         def t_sa(e):
             if ok(e):
-                turn(e, "sb", sa_t[e % 2], "e1")
+                turn(e, "sb", [sa_t[e % 2][:, i * POS:i * POS + P] for i in range(UB)], "e1")
 
         def mins(e):
             if not ok(e):
@@ -284,11 +289,11 @@ def tile_corr_t_kernel(tc, xp, xq, alpha, out_0, out_1, out_2, out_3):
                 return
             rs = live[("rs", e)]
             e2 = live[("e2", e)]
-            nc.vector.tensor_tensor(out=img(f2_t[e % 2][:, 0:EW]), in0=img(e2[:]), in1=rs[:, UB:2 * UB].unsqueeze(2).to_broadcast([P, UB, POS]), op=ALU.mult)
+            nc.vector.tensor_tensor(out=f2_t[e % 2][:, :, 0:POS], in0=img(e2[:]), in1=rs[:, UB:2 * UB].unsqueeze(2).to_broadcast([P, UB, POS]), op=ALU.mult)
 
         def t_f2(e):
             if ok(e):
-                turn(e, "f2T", f2_t[e % 2], "e2")
+                turn(e, "f2T", [f2_t[e % 2][:, i, :] for i in range(UB)], "e2")
 
         def stt(e):
             if not ok(e):
@@ -297,15 +302,16 @@ def tile_corr_t_kernel(tc, xp, xq, alpha, out_0, out_1, out_2, out_3):
             e1 = live[("e1", e)]
             f2T = live[("f2T", e)]
             for i in range(UB):
-                nc.vector.scalar_tensor_tensor(out=xa_t[e % 2][:, i * POS:(i + 1) * POS],
+                nc.vector.scalar_tensor_tensor(out=xa_t[e % 2][:, i, 0:POS],
                                                in0=e1[:, i * POS:(i + 1) * POS], scalar=rs[:, i:i + 1],
                                                in1=f2T[:, i, 0:POS], op0=ALU.mult, op1=ALU.mult)
 
         def t_xa(e):
             if not ok(e):
                 return
-            turn(e, "xbT", xa_t[e % 2], "e0")
-            store(out_3[e * UB:(e + 1) * UB].rearrange("b p k l -> p b (k l)"), img(xa_t[e % 2][0:POS, 0:EW]))
+            turn(e, "xbT", [xa_t[e % 2][:, i, :] for i in range(UB)], "e0")
+            store(out_3[e * UB:(e + 1) * UB].rearrange("b p k l -> p b (k l)"), xa_t[e % 2][0:POS, :, 0:POS])
+            vals(out_0, e - 1, xa_t[e % 2][POS:POS + BL, :, 0:POS])
 
         def cp_xb(e):
             if not ok(e):
@@ -313,19 +319,32 @@ def tile_corr_t_kernel(tc, xp, xq, alpha, out_0, out_1, out_2, out_3):
             xb = work.tile([P, EW], F32, name="xb")
             nc.vector.tensor_copy(out=img(xb[:]), in_=live[("xbT", e)][:, :, 0:POS])
             store(out_2[e * UB:(e + 1) * UB].rearrange("b q i j -> q b (i j)"), img(xb[0:POS, :]))
+            vals(out_1, e - 1, img(xb[POS:POS + BL, :]))
             live[("xb", e)] = xb
 
         def pool(e, side):
             if not ok(e):
                 return
-            srcx = xa_t[e % 2] if side == 0 else live[("xb", e)]
-            nc.vector.tensor_reduce(
-                out=pl_t[e % 2][:, side, 0:UB * 25].rearrange("p (m t) -> p m t", t=5),
-                in_=srcx[:, 0:EW].rearrange("p (m dk t dl) -> p m t dk dl", dk=2, t=5, dl=2),
-                axis=AX.XY, op=ALU.max)
+            if side == 0:
+                parts = [(xa_t[e % 2][:, i, 0:POS], i * BL, BL) for i in range(UB)]
+            else:
+                parts = [(live[("xb", e)][:], 0, UB * BL)]
+            for src, c0, n in parts:
+                nc.vector.tensor_reduce(
+                    out=pl_t[e % 2][:, side, c0:c0 + n].rearrange("p (m t) -> p m t", t=5),
+                    in_=src.rearrange("p (m dk t dl) -> p m t dk dl", dk=2, t=5, dl=2),
+                    axis=AX.XY, op=ALU.max)
+
+        def carry(e, side):
+            if not ok(e) or not ok(e + 1):
+                return
+            dst = f2_t[(e + 1) % 2] if side == 0 else xa_t[(e + 1) % 2]
+            nc.scalar.activation(out=dst[:, :, POS:POS + BL],
+                                 in_=pl_t[e % 2][:, side, 0:UB * BL].rearrange("p (b c) -> p b c", c=BL),
+                                 func=ACT.Copy, scale=float(POS) if side == 0 else 1.0)
 
         def t_pl(e):
-            if not ok(e):
+            if e != NU - 1:
                 return
             plT = pone.tile([P, 2, P], F32, name="plT", tag="e1")
             for side in range(2):
@@ -333,12 +352,12 @@ def tile_corr_t_kernel(tc, xp, xq, alpha, out_0, out_1, out_2, out_3):
             live[("plT", e)] = plT
 
         def cp_vals(e):
-            if not ok(e):
+            if e != NU - 1:
                 return
-            vals = work.tile([P, 2, POS], F32, name="vals")
-            nc.vector.tensor_copy(out=vals[:], in_=live[("plT", e)][:, :, 0:POS])
-            store(out_0[e * UB:(e + 1) * UB].rearrange("b c i j -> (b c) (i j)"), vals[0:UB * 25, 0, :])
-            store(out_1[e * UB:(e + 1) * UB].rearrange("b c k l -> (b c) (k l)"), vals[0:UB * 25, 1, :])
+            last = work.tile([P, 2, POS], F32, name="last")
+            nc.vector.tensor_copy(out=last[:], in_=live[("plT", e)][:, :, 0:POS])
+            store(out_0[e * UB:(e + 1) * UB].rearrange("b c i j -> (b c) (i j)"), last[0:UB * BL, 0, :])
+            store(out_1[e * UB:(e + 1) * UB].rearrange("b c k l -> (b c) (k l)"), last[0:UB * BL, 1, :])
 
         def window():
             gg = const.tile([P, 2, 10], F32, name="gg")
@@ -364,6 +383,7 @@ def tile_corr_t_kernel(tc, xp, xq, alpha, out_0, out_1, out_2, out_3):
                 gmult(k, PP)
                 mult(k, PP, 0)
                 sq(k + 1, PP, 0)
+                carry(k - 3, 1)
                 cp_vals(k - 3)
                 mult(k, PP, 1)
                 tr(k + 1, PP, 3)
@@ -395,6 +415,7 @@ def tile_corr_t_kernel(tc, xp, xq, alpha, out_0, out_1, out_2, out_3):
                 mult(k, QQ, 0)
                 mult(k, QQ, 1)
                 sq(k + 1, QQ, 1)
+                carry(k - 2, 0)
                 recip(k - 1)
                 tr(k + 2, PP, 0)
                 mult(k, QQ, 2)

@@ -168,14 +168,14 @@ def tile_corr_t_kernel(tc, xp, xq, alpha, out_0, out_1, out_2, out_3):
                 norm(k, o, 0, UB)
 
         def rbs(k, o):
-            if not ok(k):
+            if not (0 < k < NU):
                 return
             rc = work.tile([P, 2, POS], F32, name="rc", tag="rc%d" % o)
             nc.vector.tensor_copy(out=rc[:], in_=live[("rb", k, o)][:, UB - 2:UB, 0:POS])
             live[("rc", k, o)] = rc
 
         def gmult(k, o):
-            if not ok(k):
+            if not (0 < k < NU):
                 return
             x = xt[o][k % NXB]
             for i, g0 in ((UB - 1, 0), (UB - 2, 1)):
@@ -197,7 +197,7 @@ def tile_corr_t_kernel(tc, xp, xq, alpha, out_0, out_1, out_2, out_3):
             if not ok(k):
                 return
             x = xt[o][k % NXB]
-            for g in range(1 if i == UB - 2 else 2):
+            for g in range(1 if i == UB - 2 and k > 0 else 2):
                 c0 = (i * 2 + g) * 4 * POS
                 nc.vector.tensor_tensor(
                     out=yt[o][:, i, g, 0:POS, :].rearrange("p (c n) j -> p c j n", n=4),
@@ -289,7 +289,13 @@ def tile_corr_t_kernel(tc, xp, xq, alpha, out_0, out_1, out_2, out_3):
                 return
             rs = live[("rs", e)]
             e2 = live[("e2", e)]
-            nc.vector.tensor_tensor(out=f2_t[e % 2][:, :, 0:POS], in0=img(e2[:]), in1=rs[:, UB:2 * UB].unsqueeze(2).to_broadcast([P, UB, POS]), op=ALU.mult)
+            if e < NU - 2:
+                nc.vector.tensor_tensor(out=f2_t[e % 2][:, :, 0:POS], in0=img(e2[:]),
+                                        in1=rs[:, UB:2 * UB].unsqueeze(2).to_broadcast([P, UB, POS]), op=ALU.mult)
+                return
+            for i in range(UB):
+                nc.scalar.activation(out=f2_t[e % 2][:, i, 0:POS], in_=e2[:, i * POS:(i + 1) * POS], func=ACT.Copy,
+                                     scale=rs[:, UB + i:UB + i + 1])
 
         def t_f2(e):
             if ok(e):
@@ -317,7 +323,8 @@ def tile_corr_t_kernel(tc, xp, xq, alpha, out_0, out_1, out_2, out_3):
             if not ok(e):
                 return
             xb = work.tile([P, EW], F32, name="xb")
-            nc.vector.tensor_copy(out=img(xb[:]), in_=live[("xbT", e)][:, :, 0:POS])
+            copy = nc.vector.tensor_copy if e < NU - 3 else nc.scalar.copy
+            copy(out=img(xb[:]), in_=live[("xbT", e)][:, :, 0:POS])
             store(out_2[e * UB:(e + 1) * UB].rearrange("b q i j -> q b (i j)"), img(xb[0:POS, :]))
             vals(out_1, e - 1, img(xb[POS:POS + BL, :]))
             live[("xb", e)] = xb
@@ -396,6 +403,8 @@ def tile_corr_t_kernel(tc, xp, xq, alpha, out_0, out_1, out_2, out_3):
                 sq(k + 1, PP, 2)
                 t_xa(k - 2)
                 mult(k, PP, 2)
+                if k == 0:
+                    mult(k, PP, 3)
                 rbs(k, QQ)
                 tr(k + 1, QQ, 1)
                 sq(k + 1, PP, 3)
@@ -419,6 +428,8 @@ def tile_corr_t_kernel(tc, xp, xq, alpha, out_0, out_1, out_2, out_3):
                 recip(k - 1)
                 tr(k + 2, PP, 0)
                 mult(k, QQ, 2)
+                if k == 0:
+                    mult(k, QQ, 3)
                 sq(k + 1, QQ, 2)
                 tr(k + 2, PP, 1)
                 sq(k + 1, QQ, 3)

@@ -35,7 +35,7 @@ def tile_corr_t_kernel(tc, xp, xq, alpha, out_0, out_1, out_2, out_3):
             tc.tile_pool(name="fixed", bufs=1) as fixed, \
             tc.tile_pool(name="work", bufs=2) as work, \
             tc.tile_pool(name="small", bufs=4) as small, \
-            tc.psum_pool(name="pxt", bufs=3) as pxt, \
+            tc.psum_pool(name="pxt", bufs=4) as pxt, \
             tc.psum_pool(name="pone", bufs=1) as pone:
         ident_b = const.tile([P, P], BF16, name="ident_b")
         make_identity(nc, ident_b[:])
@@ -299,7 +299,7 @@ def tile_corr_t_kernel(tc, xp, xq, alpha, out_0, out_1, out_2, out_3):
 
         def t_f2(e):
             if ok(e):
-                turn(e, "f2T", [f2_t[e % 2][:, i, :] for i in range(UB)], "e2")
+                turn(e, "f2T", [f2_t[e % 2][:, i, :] for i in range(UB)], "e1")
 
         def stt(e):
             if not ok(e):
@@ -393,22 +393,22 @@ def tile_corr_t_kernel(tc, xp, xq, alpha, out_0, out_1, out_2, out_3):
                 carry(k - 3, 1)
                 cp_vals(k - 3)
                 mult(k, PP, 1)
-                tr(k + 1, PP, 3)
+                tr(k + 1, QQ, 0)
                 bcast(k, QQ)
                 sq(k + 1, PP, 1)
-                mask(k - 1)
                 stt(k - 2)
+                mask(k - 1)
                 t_sa(k - 1)
-                tr(k + 1, QQ, 0)
+                tr(k + 1, QQ, 1)
                 sq(k + 1, PP, 2)
                 t_xa(k - 2)
                 mult(k, PP, 2)
                 if k == 0:
                     mult(k, PP, 3)
                 rbs(k, QQ)
-                tr(k + 1, QQ, 1)
-                sq(k + 1, PP, 3)
                 tr(k + 1, QQ, 2)
+                sq(k + 1, PP, 3)
+                tr(k + 1, QQ, 3)
                 if k == -1:
                     window()
                 powr(k + 1, PP)
@@ -416,7 +416,7 @@ def tile_corr_t_kernel(tc, xp, xq, alpha, out_0, out_1, out_2, out_3):
                 sq(k + 1, QQ, 0)
                 quant(k, PP)
                 gmult(k, QQ)
-                tr(k + 1, QQ, 3)
+                tr(k + 2, PP, 0)
                 exps(k - 1)
                 bcast(k + 1, PP)
                 pool(k - 2, 0)
@@ -426,17 +426,17 @@ def tile_corr_t_kernel(tc, xp, xq, alpha, out_0, out_1, out_2, out_3):
                 sq(k + 1, QQ, 1)
                 carry(k - 2, 0)
                 recip(k - 1)
-                tr(k + 2, PP, 0)
+                tr(k + 2, PP, 1)
                 mult(k, QQ, 2)
                 if k == 0:
                     mult(k, QQ, 3)
                 sq(k + 1, QQ, 2)
-                tr(k + 2, PP, 1)
+                tr(k + 2, PP, 2)
                 sq(k + 1, QQ, 3)
                 f2s(k - 1)
                 t_f2(k - 1)
                 pool(k - 2, 1)
                 t_pl(k - 2)
-                tr(k + 2, PP, 2)
+                tr(k + 2, PP, 3)
                 quant(k, QQ)
                 rbs(k + 1, PP)

import concourse.mybir as mybir
from concourse.masks import make_identity

FLOPS = 2 * 64 * 100 * 100 * 1024

BF16 = mybir.dt.bfloat16
F32 = mybir.dt.float32
I32 = mybir.dt.int32
U32 = mybir.dt.uint32
U8 = mybir.dt.uint8
FP8X4 = mybir.dt.float8_e4m3fn_x4
ALU = mybir.AluOpType
ACT = mybir.ActivationFunctionType
AX = mybir.AxisListType

P = 128
B = 64
POS = 100
UB = 4
NU = B // UB
CH = 8
XW = UB * CH * POS
PADW = P - POS
EW = UB * POS
BL = 25
NXB = 4
EPS2 = 1e-24
PP = 0
QQ = 1


def tile_corr_t_kernel(tc, xp, xq, alpha, out_0, out_1, out_2, out_3):
    nc = tc.nc
    with tc.tile_pool(name="const", bufs=1) as const, \
            tc.tile_pool(name="fixed", bufs=1) as fixed, \
            tc.tile_pool(name="work", bufs=2) as work, \
            tc.tile_pool(name="small", bufs=4) as small, \
            tc.psum_pool(name="pxt", bufs=4) as pxt, \
            tc.psum_pool(name="pone", bufs=1) as pone:
        ident_b = const.tile([P, P], BF16, name="ident_b")
        make_identity(nc, ident_b[:])
        ident_f = const.tile([P, P], F32, name="ident_f")
        make_identity(nc, ident_f[:])
        neg_half = const.tile([P, UB], F32, name="neg_half")
        nc.gpsimd.memset(neg_half[:], -0.5)
        first = const.tile([P, 1], F32, name="first")
        nc.scalar.activation(out=first[:], in_=neg_half[:, 0:1], func=ACT.Exp)
        wneg = const.tile([P, POS], F32, name="wneg")
        junk = const.tile([P, CH * P], BF16, name="junk")

        xt = [[fixed.tile([P, XW + 32], BF16, name="x%d_%d" % (o, k)) for k in range(NXB)] for o in range(2)]
        yt = [fixed.tile([P, UB, 2, P, 4], BF16, name="y%d" % o, align_bytes=64) for o in range(2)]
        sa_t = [fixed.tile([P, EW + PADW], F32, name="sa%d" % k) for k in range(2)]
        f2_t = [fixed.tile([P, UB, P], F32, name="f2%d" % k) for k in range(2)]
        xa_t = [fixed.tile([P, UB, P], F32, name="xa%d" % k) for k in range(2)]
        pl_t = [fixed.tile([P, 2, P], F32, name="pl%d" % k) for k in range(2)]
        for o in range(2):
            for k in range(NXB):
                nc.vector.memset(xt[o][k][:, XW:XW + 32], 0.0)
            nc.vector.memset(yt[o][:, :, :, POS:P, :], 0.0)
        for k in range(2):
            nc.gpsimd.memset(sa_t[k][:, EW:EW + PADW], 0.0)
            nc.gpsimd.memset(f2_t[k][:, :, POS:P], 0.0)
            nc.gpsimd.memset(xa_t[k][:, :, POS:P], 0.0)
            nc.gpsimd.memset(pl_t[k][:], 0.0)

        a_bf = const.tile([P, 1], BF16, name="a_bf")
        nc.scalar.dma_start(out=a_bf[:], in_=alpha.partition_broadcast(P))
        pi = const.tile([P, 1], I32, name="pi")
        nc.gpsimd.iota(pi[:], pattern=[[0, 1]], base=0, channel_multiplier=1)
        ti = const.tile([P, 12], I32, name="ti")
        nc.gpsimd.iota(ti[:], pattern=[[10, 12]], base=10, channel_multiplier=0)
        ki = const.tile([P, 10], I32, name="ki")
        nc.gpsimd.iota(ki[:], pattern=[[1, 10]], base=0, channel_multiplier=0)
        pf = const.tile([P, 1], F32, name="pf")
        nc.vector.tensor_copy(out=pf[:], in_=pi[:])
        tf = const.tile([P, 12], F32, name="tf")
        nc.vector.tensor_copy(out=tf[:], in_=ti[:])
        kf = const.tile([P, 10], F32, name="kf")
        nc.vector.tensor_copy(out=kf[:], in_=ki[:])
        ge = const.tile([P, 12], F32, name="ge")
        nc.vector.tensor_scalar(out=ge[:], in0=tf[:], scalar1=pf[:, 0:1], scalar2=None, op0=ALU.is_le)
        irow = const.tile([P, 1], F32, name="irow")
        nc.vector.tensor_reduce(out=irow[:], in_=ge[:], axis=AX.X, op=ALU.add)
        jcol = const.tile([P, 1], F32, name="jcol")
        nc.vector.scalar_tensor_tensor(out=jcol[:], in0=irow[:], scalar=-10.0, in1=pf[:],
                                       op0=ALU.mult, op1=ALU.add)
        dd = const.tile([P, 2, 10], F32, name="dd")
        nc.vector.tensor_scalar(out=dd[:, 0, :], in0=kf[:], scalar1=irow[:, 0:1], scalar2=None,
                                op0=ALU.subtract)
        nc.vector.tensor_scalar(out=dd[:, 1, :], in0=kf[:], scalar1=jcol[:, 0:1], scalar2=None,
                                op0=ALU.subtract)
        d2 = const.tile([P, 2, 10], F32, name="d2")
        nc.vector.tensor_tensor(out=d2[:], in0=dd[:], in1=dd[:], op=ALU.mult)

        live = {}

        def ok(k):
            return 0 <= k < NU

        def img(ap):
            return ap.rearrange("p (b q) -> p b q", b=UB)

        def store(dst, src):
            for lo, hi in ((0, 64), (64, 96), (96, 100)):
                nc.sync.dma_start(out=dst[lo:hi], in_=src[lo:hi])

        def vals(dst, e, rows):
            if ok(e):
                nc.sync.dma_start(out=dst[e * UB:(e + 1) * UB].rearrange("b c i j -> c b (i j)"), in_=rows)

        def load(k, o):
            if not ok(k):
                return
            src = xp if o == PP else xq
            step = 1 if k == 0 else UB
            for i in range(0, UB, step):
                nc.sync.dma_start(
                    out=xt[o][k % NXB][:, i * CH * POS:(i + step) * CH * POS].rearrange(
                        "p (n f) -> p n f", n=2 * step),
                    in_=src[k * UB + i:k * UB + i + step].rearrange(
                        "b (g p j) h w -> p (b g) (j h w)", g=2, p=P, j=4),
                )

        def tr(k, o, i):
            if not ok(k):
                return
            x = xt[o][k % NXB]
            xT = pxt.tile([P, CH * P], BF16, name="xT")
            for t in range(CH):
                c0 = (i * CH + t) * POS
                nc.tensor.transpose(xT[:, t * P:(t + 1) * P], x[:, c0:c0 + P], ident_b[:])
            live[("xT", k, o, i)] = xT

        def sq(k, o, i):
            if not ok(k):
                return
            if i == 0:
                n2 = small.tile([P, UB], F32, name="n2")
                live[("n2", k, o)] = n2
            nc.scalar.activation(out=junk[:], in_=live[("xT", k, o, i)][:], func=ACT.Square,
                                 accum_out=live[("n2", k, o)][:, i:i + 1])
            if k == 0:
                norm(k, o, i, i + 1)
                spread(k, o, i, i + 1)

        def norm(k, o, lo, hi):
            if lo == 0:
                n2c = small.tile([P, UB], F32, name="n2c")
                rn = small.tile([P, UB], F32, name="rn")
                live[("n2c", k, o)] = n2c
                live[("rn", k, o)] = rn
            nc.gpsimd.tensor_scalar_max(out=live[("n2c", k, o)][:, lo:hi], in0=live[("n2", k, o)][:, lo:hi],
                                        scalar1=EPS2)
            nc.gpsimd.tensor_tensor(out=live[("rn", k, o)][:, lo:hi], in0=live[("n2c", k, o)][:, lo:hi],
                                    in1=neg_half[:, lo:hi], op=ALU.pow)

        def spread(k, o, lo, hi):
            if lo == 0:
                rb = pone.tile([P, UB, P], F32, name="rb", tag="rb%d" % o)
                live[("rb", k, o)] = rb
            for i in range(lo, hi):
                nc.tensor.transpose(live[("rb", k, o)][:, i, :],
                                    live[("rn", k, o)][:, i:i + 1].to_broadcast([P, P]), ident_f[:])

        def powr(k, o):
            if 0 < k < NU:
                norm(k, o, 0, UB)

        def rbs(k, o):
            if not (0 < k < NU):
                return
            rc = work.tile([P, 2, POS], F32, name="rc", tag="rc%d" % o)
            nc.vector.tensor_copy(out=rc[:], in_=live[("rb", k, o)][:, UB - 2:UB, 0:POS])
            live[("rc", k, o)] = rc

        def gmult(k, o):
            if not (0 < k < NU):
                return
            x = xt[o][k % NXB]
            for i, g0 in ((UB - 1, 0), (UB - 2, 1)):
                ng = 2 - g0
                c0 = (i * 2 + g0) * 4 * POS
                nc.gpsimd.tensor_tensor(
                    out=yt[o][:, i, g0:2, 0:POS, :],
                    in0=x[:, c0:c0 + ng * 4 * POS].rearrange("p (g j w) -> p g w j", g=ng, j=4),
                    in1=live[("rc", k, o)][:, i - UB + 2, :].unsqueeze(1).unsqueeze(3).to_broadcast(
                        [P, ng, POS, 4]),
                    op=ALU.mult,
                )

        def bcast(k, o):
            if 0 < k < NU:
                spread(k, o, 0, UB)

        def mult(k, o, i):
            if not ok(k):
                return
            x = xt[o][k % NXB]
            for g in range(1 if i == UB - 2 and k > 0 else 2):
                c0 = (i * 2 + g) * 4 * POS
                nc.vector.tensor_tensor(
                    out=yt[o][:, i, g, 0:POS, :].rearrange("p (c n) j -> p c j n", n=4),
                    in0=x[:, c0:c0 + 4 * POS].rearrange("p (j c n) -> p c j n", j=4, n=4),
                    in1=live[("rb", k, o)][:, i, 0:POS].rearrange("p (c n) -> p c n", n=4).unsqueeze(2).to_broadcast(
                        [P, POS // 4, 4, 4]),
                    op=ALU.mult,
                )

        def quant(k, o):
            if not ok(k):
                return
            cw = work.tile([P, UB * 2 * P], U32, name="cw", tag="cw%d" % o, align_bytes=64)
            cs = work.tile([P, UB * 2 * P], U8, name="cs", tag="cs%d" % o, align_bytes=64)
            nc.vector.quantize_mx(out=cw[:].bitcast(FP8X4), scales=cs[:],
                                  in_=yt[o][:].rearrange("p b g w j -> p (b g w j)"))
            live[("c", k, o)] = (cw, cs)

        def mx(e):
            if not ok(e):
                return
            cwp, csp = live[("c", e, PP)]
            cwq, csq = live[("c", e, QQ)]
            aff = pone.tile([P, UB, P], F32, name="aff", tag="e0")
            for i in range(UB):
                for g in range(2):
                    cols = slice((i * 2 + g) * P, (i * 2 + g + 1) * P)
                    nc.tensor.matmul_mx(out=aff[:, i, :],
                                        lhsT=cwp[:, cols].bitcast(FP8X4), lhsT_scale=csp[:, cols],
                                        rhs=cwq[:, cols].bitcast(FP8X4), rhs_scale=csq[:, cols],
                                        start=(g == 0), stop=(g == 1))
            live[("aff", e)] = aff

        def mask(e):
            if not ok(e):
                return
            nc.vector.tensor_tensor(out=img(sa_t[e % 2][:, 0:EW]), in0=live[("aff", e)][:, :, 0:POS],
                                    in1=wneg[:].unsqueeze(1).to_broadcast([P, UB, POS]), op=ALU.mult)

        def turn(e, key, windows, tag):
            dst = pone.tile([P, UB, P], F32, name=key, tag=tag)
            for i in range(UB):
                nc.tensor.transpose(dst[:, i, :], windows[i], ident_f[:])
            live[(key, e)] = dst

        def t_sa(e):
            if ok(e):
                turn(e, "sb", [sa_t[e % 2][:, i * POS:i * POS + P] for i in range(UB)], "e1")

        def mins(e):
            if not ok(e):
                return
            nm = small.tile([P, 2 * UB], F32, name="nm")
            nc.vector.tensor_reduce(out=nm[:, 0:UB], in_=img(sa_t[e % 2][:, 0:EW]), axis=AX.X, op=ALU.min)
            nc.vector.tensor_reduce(out=nm[:, UB:2 * UB], in_=live[("sb", e)][:, :, 0:POS], axis=AX.X,
                                    op=ALU.min)
            live[("nm", e)] = nm

        def exps(e):
            if not ok(e):
                return
            nm = live[("nm", e)]
            sa = sa_t[e % 2]
            sb = live[("sb", e)]
            e1 = work.tile([P, EW], F32, name="e1")
            e2 = work.tile([P, EW], F32, name="e2")
            sm = small.tile([P, 2 * UB], F32, name="sm")
            for i in range(UB):
                nc.scalar.activation(out=e1[:, i * POS:(i + 1) * POS], in_=sa[:, i * POS:(i + 1) * POS],
                                     func=ACT.Exp, bias=nm[:, i:i + 1], scale=-1.0,
                                     accum_out=sm[:, i:i + 1])
            for i in range(UB):
                nc.scalar.activation(out=e2[:, i * POS:(i + 1) * POS], in_=sb[:, i, 0:POS],
                                     func=ACT.Exp, bias=nm[:, UB + i:UB + i + 1], scale=-1.0,
                                     accum_out=sm[:, UB + i:UB + i + 1])
            live[("e1", e)] = e1
            live[("e2", e)] = e2
            live[("sm", e)] = sm

        def recip(e):
            if not ok(e):
                return
            rs = small.tile([P, 2 * UB], F32, name="rs")
            nc.vector.reciprocal(out=rs[:], in_=live[("sm", e)][:])
            live[("rs", e)] = rs

        def f2s(e):
            if not ok(e):
                return
            rs = live[("rs", e)]
            e2 = live[("e2", e)]
            if e < NU - 2:
                nc.vector.tensor_tensor(out=f2_t[e % 2][:, :, 0:POS], in0=img(e2[:]),
                                        in1=rs[:, UB:2 * UB].unsqueeze(2).to_broadcast([P, UB, POS]), op=ALU.mult)
                return
            for i in range(UB):
                nc.scalar.activation(out=f2_t[e % 2][:, i, 0:POS], in_=e2[:, i * POS:(i + 1) * POS], func=ACT.Copy,
                                     scale=rs[:, UB + i:UB + i + 1])

        def t_f2(e):
            if ok(e):
                turn(e, "f2T", [f2_t[e % 2][:, i, :] for i in range(UB)], "e1")

        def stt(e):
            if not ok(e):
                return
            rs = live[("rs", e)]
            e1 = live[("e1", e)]
            f2T = live[("f2T", e)]
            for i in range(UB):
                nc.vector.scalar_tensor_tensor(out=xa_t[e % 2][:, i, 0:POS],
                                               in0=e1[:, i * POS:(i + 1) * POS], scalar=rs[:, i:i + 1],
                                               in1=f2T[:, i, 0:POS], op0=ALU.mult, op1=ALU.mult)

        def t_xa(e):
            if not ok(e):
                return
            turn(e, "xbT", [xa_t[e % 2][:, i, :] for i in range(UB)], "e0")
            store(out_3[e * UB:(e + 1) * UB].rearrange("b p k l -> p b (k l)"), xa_t[e % 2][0:POS, :, 0:POS])
            vals(out_0, e - 1, xa_t[e % 2][POS:POS + BL, :, 0:POS])

        def cp_xb(e):
            if not ok(e):
                return
            xb = work.tile([P, EW], F32, name="xb")
            copy = nc.vector.tensor_copy if e < NU - 3 else nc.scalar.copy
            copy(out=img(xb[:]), in_=live[("xbT", e)][:, :, 0:POS])
            store(out_2[e * UB:(e + 1) * UB].rearrange("b q i j -> q b (i j)"), img(xb[0:POS, :]))
            vals(out_1, e - 1, img(xb[POS:POS + BL, :]))
            live[("xb", e)] = xb

        def pool(e, side):
            if not ok(e):
                return
            if side == 0:
                parts = [(xa_t[e % 2][:, i, 0:POS], i * BL, BL) for i in range(UB)]
            else:
                parts = [(live[("xb", e)][:], 0, UB * BL)]
            for src, c0, n in parts:
                nc.vector.tensor_reduce(
                    out=pl_t[e % 2][:, side, c0:c0 + n].rearrange("p (m t) -> p m t", t=5),
                    in_=src.rearrange("p (m dk t dl) -> p m t dk dl", dk=2, t=5, dl=2),
                    axis=AX.XY, op=ALU.max)

        def carry(e, side):
            if not ok(e) or not ok(e + 1):
                return
            dst = f2_t[(e + 1) % 2] if side == 0 else xa_t[(e + 1) % 2]
            nc.scalar.activation(out=dst[:, :, POS:POS + BL],
                                 in_=pl_t[e % 2][:, side, 0:UB * BL].rearrange("p (b c) -> p b c", c=BL),
                                 func=ACT.Copy, scale=float(POS) if side == 0 else 1.0)

        def t_pl(e):
            if e != NU - 1:
                return
            plT = pone.tile([P, 2, P], F32, name="plT", tag="e1")
            for side in range(2):
                nc.tensor.transpose(plT[:, side, :], pl_t[e % 2][:, side, :], ident_f[:])
            live[("plT", e)] = plT

        def cp_vals(e):
            if e != NU - 1:
                return
            last = work.tile([P, 2, POS], F32, name="last")
            nc.vector.tensor_copy(out=last[:], in_=live[("plT", e)][:, :, 0:POS])
            store(out_0[e * UB:(e + 1) * UB].rearrange("b c i j -> (b c) (i j)"), last[0:UB * BL, 0, :])
            store(out_1[e * UB:(e + 1) * UB].rearrange("b c k l -> (b c) (k l)"), last[0:UB * BL, 1, :])

        def window():
            gg = const.tile([P, 2, 10], F32, name="gg")
            nc.scalar.activation(out=gg[:], in_=d2[:], func=ACT.Exp, scale=-2.0)
            g2 = const.tile([P, 10, 10], F32, name="g2")
            nc.vector.tensor_tensor(out=g2[:],
                                    in0=gg[:, 0, :].unsqueeze(2).to_broadcast([P, 10, 10]),
                                    in1=gg[:, 1, :].unsqueeze(1).to_broadcast([P, 10, 10]),
                                    op=ALU.mult)
            a_f = const.tile([P, 1], F32, name="a_f")
            nc.vector.tensor_copy(out=a_f[:], in_=a_bf[:])
            wm1 = const.tile([P, POS], F32, name="wm1")
            nc.vector.tensor_scalar(out=wm1[:], in0=g2[:].rearrange("p k l -> p (k l)"), scalar1=1.0,
                                    scalar2=None, op0=ALU.subtract)
            nc.vector.tensor_scalar(out=wneg[:], in0=wm1[:], scalar1=a_f[:, 0:1], scalar2=None, op0=ALU.mult)

        with tc.manual_schedule():
            for k in range(-3, NU + 3):
                load(k + 3, PP)
                load(k + 3, QQ)
                mx(k - 1)
                powr(k, QQ)
                gmult(k, PP)
                mult(k, PP, 0)
                sq(k + 1, PP, 0)
                carry(k - 3, 1)
                cp_vals(k - 3)
                mult(k, PP, 1)
                tr(k + 1, QQ, 0)
                bcast(k, QQ)
                sq(k + 1, PP, 1)
                stt(k - 2)
                mask(k - 1)
                t_sa(k - 1)
                tr(k + 1, QQ, 1)
                sq(k + 1, PP, 2)
                t_xa(k - 2)
                mult(k, PP, 2)
                if k == 0:
                    mult(k, PP, 3)
                rbs(k, QQ)
                tr(k + 1, QQ, 2)
                sq(k + 1, PP, 3)
                tr(k + 1, QQ, 3)
                if k == -1:
                    window()
                powr(k + 1, PP)
                mins(k - 1)
                sq(k + 1, QQ, 0)
                quant(k, PP)
                gmult(k, QQ)
                tr(k + 2, PP, 0)
                exps(k - 1)
                bcast(k + 1, PP)
                pool(k - 2, 0)
                cp_xb(k - 2)
                mult(k, QQ, 0)
                mult(k, QQ, 1)
                sq(k + 1, QQ, 1)
                carry(k - 2, 0)
                recip(k - 1)
                tr(k + 2, PP, 1)
                mult(k, QQ, 2)
                if k == 0:
                    mult(k, QQ, 3)
                sq(k + 1, QQ, 2)
                tr(k + 2, PP, 2)
                sq(k + 1, QQ, 3)
                f2s(k - 1)
                t_f2(k - 1)
                pool(k - 2, 1)
                t_pl(k - 2)
                tr(k + 2, PP, 3)
                quant(k, QQ)
                rbs(k + 1, PP)
